import numpy as np
import ml_dtypes


def mxq(x, axis, fmt="e4m3"):
    dtype, down = {"e4m3": (ml_dtypes.float8_e4m3fn, 7), "e5m2": (ml_dtypes.float8_e5m2, 14)}[fmt]
    v = np.moveaxis(np.asarray(x, np.float32).astype(ml_dtypes.bfloat16).astype(np.float64), axis, -1)
    blocks = v.reshape(v.shape[:-1] + (-1, 32))
    amax = np.abs(blocks).max(-1, keepdims=True)
    byte = np.maximum(np.where(amax > 0, np.frexp(amax)[1] - 1 + 127, 0) - down, 1)
    scale = np.exp2(byte - 127.0)
    codes = (blocks / scale).astype(np.float32).astype(dtype).astype(np.float64)
    return np.moveaxis((codes * scale).reshape(v.shape), -1, axis)


WIDE = False


def mx_kscale(k):
    if not WIDE:
        return np.ones(k)
    levels = np.array([10, -10, 5, -5, 0])
    if k % 512:
        return np.exp2(np.random.permutation(np.resize(levels, k // 32))).repeat(32)
    a = np.empty((k // 512, 16))
    for p in range(k // 512):
        a[p, :8] = np.random.permutation(np.resize(levels, 8))
        for g in range(8):
            far = levels[np.abs(levels - a[p, g]) >= 10]
            a[p, g + 8] = far[np.random.randint(len(far))]
    return np.exp2(a.ravel()).repeat(32)


BF16 = ml_dtypes.bfloat16


def bf(x):
    return np.asarray(x, np.float32).astype(BF16)


def f64(x):
    return np.asarray(x).astype(np.float64)


B, S, D, E = 2, 512, 512, 512
SC = 1.5


def draw0():
    s, t = mx_kscale(D), mx_kscale(E)
    rn = np.random.standard_normal
    qs = np.sqrt(SC / np.sqrt(2.0 * E))
    ws = qs / np.sqrt(2.0 * D)
    return {"x_re": bf(rn((B, S, D)) * s), "x_im": bf(rn((B, S, D)) * s),
            "Wq_re": bf(rn((E, D)) * ws * t[:, None] / s), "Wq_im": bf(rn((E, D)) * ws * t[:, None] / s),
            "bq_re": bf(rn(E) * 0.5 * qs * t), "bq_im": bf(rn(E) * 0.5 * qs * t),
            "Wk_re": bf(rn((E, D)) * ws / t[:, None] / s), "Wk_im": bf(rn((E, D)) * ws / t[:, None] / s),
            "bk_re": bf(rn(E) * 0.5 * qs / t), "bk_im": bf(rn(E) * 0.5 * qs / t)}


def cproj(xr, xi, w_re, w_im, b_re, b_im):
    wr = mxq(f64(w_re), 1, "e4m3").T
    wi = mxq(f64(w_im), 1, "e4m3").T
    y_re = (xr @ wr) - (xi @ wi) + f64(b_re)
    y_im = (xr @ wi) + (xi @ wr) + f64(b_im)
    return y_re, y_im


def core(x_re, x_im, Wq_re, Wq_im, bq_re, bq_im, Wk_re, Wk_im, bk_re, bk_im):
    xr = mxq(f64(x_re), 2, "e4m3")
    xi = mxq(f64(x_im), 2, "e4m3")
    q_re, q_im = cproj(xr, xi, Wq_re, Wq_im, bq_re, bq_im)
    k_re, k_im = cproj(xr, xi, Wk_re, Wk_im, bk_re, bk_im)
    return ((mxq(q_re, 2, "e4m3") @ mxq(k_re, 2, "e4m3").transpose(0, 2, 1))
            + (mxq(q_im, 2, "e4m3") @ mxq(k_im, 2, "e4m3").transpose(0, 2, 1)))


def e4m3fn_bytes(y):
    return np.clip(np.asarray(y, np.float64), -448.0, 448.0).astype(np.float32).astype(ml_dtypes.float8_e4m3fn).view(np.uint8)


def e4m3fn_values(b):
    return np.asarray(b, np.uint8).view(ml_dtypes.float8_e4m3fn).astype(np.float64)


def setup_inputs():
    d = draw0()
    x0 = np.asarray(d['x_re']).astype(np.float64)
    s = (np.max(np.abs(x0), axis=(0, 1), keepdims=True) / 448.0).astype(np.float32)
    out = {}
    for k, v in d.items():
        if k == 'x_re':
            out['x_re_bytes'] = e4m3fn_bytes(x0 / s.astype(np.float64))
            out['x_re_scale'] = s
        else:
            out[k] = v
    return out


def reference(x_re_bytes, x_re_scale, x_im, Wq_re, Wq_im, bq_re, bq_im, Wk_re, Wk_im, bk_re, bk_im):
    return core(e4m3fn_values(x_re_bytes) * x_re_scale.astype(np.float64), x_im, Wq_re, Wq_im, bq_re, bq_im, Wk_re, Wk_im, bk_re, bk_im)

@@ -1,0 +1,229 @@
+from contextlib import ExitStack
+
+import concourse.mybir as mybir
+from concourse.masks import make_identity
+
+FLOPS = 8 * 2 * 1024 * 512 * 512 + 2 * 2 * 2 * 512 * 512 * 512
+
+F32 = mybir.dt.float32
+BF16 = mybir.dt.bfloat16
+U32 = mybir.dt.uint32
+U8 = mybir.dt.uint8
+FP8 = mybir.dt.float8_e4m3fn
+FP8X4 = mybir.dt.float8_e4m3fn_x4
+ALU = mybir.AluOpType
+ACT = mybir.ActivationFunctionType
+
+P = 128
+K = 512
+BATCHES = 2
+
+
+def tile_teleportationattention_pa_kernel(
+    tc, x_re_bytes, x_re_scale, x_im, Wq_re, Wq_im, bq_re, bq_im, Wk_re, Wk_im, bk_re, bk_im, out
+):
+    nc = tc.nc
+    with ExitStack() as ctx:
+        keep = ctx.enter_context(tc.tile_pool(name="keep", bufs=1))
+        psum = ctx.enter_context(tc.psum_pool(name="psum", bufs=8))
+
+        def new(name, shape, dtype):
+            return keep.tile(shape, dtype, name=name, align_bytes=64)
+
+        def bank_tile():
+            return psum.tile([P, 512], F32, name="bank")
+
+        ident = new("ident", [P, P], F32)
+        dummy = new("dummy", [P, 1], F32)
+        scale_col = new("scale_col", [P, 4], F32)
+        scale_row = new("scale_row", [P, K], F32)
+        bias_in = {"qr": bq_re, "qi": bq_im, "kr": bk_re, "ki": bk_im}
+        bias = {}
+        for n in bias_in:
+            bias[n] = new("bias_" + n, [P, 4], BF16)
+
+        raw = {}
+        for n in ("wqr", "wqi", "wkr", "wki", "xr0", "xi0", "xr1", "xi1"):
+            raw[n] = new("raw_" + n, [P, 4, K], BF16)
+        xbytes = [new("xbytes%d" % b, [P, 4, K], U8) for b in range(BATCHES)]
+        grouped = {}
+        codes = {}
+        scales = {}
+        for n in ("wqr", "wqi", "wkr", "wki", "xr0", "xi0", "xn0", "xr1", "xi1", "xn1", "qr0", "qi0", "kr0", "ki0", "qr1", "qi1", "kr1", "ki1"):
+            grouped[n] = new("grp_" + n, [P, 4 * 512], BF16)
+            codes[n] = new("codes_" + n, [P, 512], U32)
+            scales[n] = new("scales_" + n, [P, 512], U8)
+        planes = {}
+        for n in ("qr0", "qi0", "kr0", "ki0", "qr1", "qi1", "kr1", "ki1"):
+            planes[n] = new("planes_" + n, [P, 4, 512], BF16)
+        result = [new("result%d" % b, [P, 4, 512], F32) for b in range(BATCHES)]
+
+        w_view = {"wqr": Wq_re, "wqi": Wq_im, "wkr": Wk_re, "wki": Wk_im}
+        src = {}
+        for n in w_view:
+            src[n] = w_view[n].rearrange("(m s) k -> m s k", s=4)
+        for b in range(BATCHES):
+            src["xi%d" % b] = x_im[b].rearrange("(m s) k -> m s k", s=4)
+
+        def load(n, parts=1):
+            step = 4 // parts
+            for i in range(parts):
+                nc.sync.dma_start(out=raw[n][:, i * step : (i + 1) * step, :], in_=src[n][:, i * step : (i + 1) * step, :])
+
+        def load_bytes(b):
+            nc.sync.dma_start(out=xbytes[b][:], in_=x_re_bytes[b].rearrange("(m s) k -> m s k", s=4))
+
+        def widen(b, s):
+            nc.vector.tensor_tensor(
+                out=raw["xr%d" % b][:, s, :], in0=xbytes[b][:, s, :].bitcast(FP8), in1=scale_row[:], op=ALU.mult
+            )
+
+        def turn(n, on_vector=()):
+            for h in range(2):
+                bank = bank_tile()
+                v = bank[:].rearrange("p (c u r) -> p c u r", c=2, u=2)
+                for c in range(2):
+                    words = raw[n][:, 2 * h + c, :].bitcast(F32)
+                    for u in range(2):
+                        nc.tensor.transpose(v[:, c, u, :], words[:, u:256:2], ident[:])
+                target = grouped[n][:, 1024 * h : 1024 * (h + 1)].bitcast(F32).rearrange("p (c r u) -> p c r u", c=2, u=2)
+                if h in on_vector:
+                    nc.vector.tensor_copy(out=target, in_=v.rearrange("p c u r -> p c r u"))
+                else:
+                    nc.scalar.copy(out=target, in_=v.rearrange("p c u r -> p c r u"))
+
+        def quant(n, h=None):
+            lo, hi = (0, 512) if h is None else (256 * h, 256 * (h + 1))
+            nc.vector.quantize_mx(
+                out=codes[n][:, lo:hi].bitcast(FP8X4), scales=scales[n][:, lo:hi], in_=grouped[n][:, 4 * lo : 4 * hi]
+            )
+
+        def negate(b):
+            nc.vector.tensor_scalar(out=grouped["xn%d" % b][:], in0=grouped["xi%d" % b][:], scalar1=-1.0, scalar2=None, op0=ALU.mult)
+
+        def mm(bank, w, t, x, start, stop):
+            nc.tensor.matmul_mx(
+                out=bank[:],
+                lhsT=codes[w][:, 128 * t : 128 * (t + 1)].bitcast(FP8X4),
+                lhsT_scale=scales[w][:, 128 * t : 128 * (t + 1)],
+                rhs=codes[x][:].bitcast(FP8X4),
+                rhs_scale=scales[x][:],
+                start=start,
+                stop=stop,
+            )
+
+        def operands(side, part, b):
+            if part == "r":
+                return [("w%sr" % side, "xr%d" % b), ("w%si" % side, "xn%d" % b)]
+            return [("w%sr" % side, "xi%d" % b), ("w%si" % side, "xr%d" % b)]
+
+        def leave(bank, side, part, b, t, engine):
+            plane = planes["%s%s%d" % (side, part, b)][:, t, :]
+            column = bias[side + part][:, t : t + 1]
+            if engine == "scalar":
+                nc.scalar.activation(out=plane, in_=bank[:], func=ACT.Identity, bias=column, scale=1.0)
+            else:
+                nc.vector.tensor_scalar(out=plane, in0=bank[:], scalar1=column, scalar2=None, op0=ALU.add)
+
+        def unit(side, part, b, on_vector=()):
+            ops = operands(side, part, b)
+            for t in range(4):
+                bank = bank_tile()
+                for i in range(2):
+                    mm(bank, ops[i][0], t, ops[i][1], i == 0, i == 1)
+                leave(bank, side, part, b, t, "vector" if t in on_vector else "scalar")
+
+        def interleave(n, h):
+            nc.vector.tensor_copy(
+                out=grouped[n][:, 1024 * h : 1024 * (h + 1)].rearrange("p (c i t) -> p c t i", i=4, t=4),
+                in_=planes[n][:, :, 256 * h : 256 * (h + 1)].rearrange("p t (c i) -> p c t i", i=4),
+            )
+
+        def pack(n):
+            interleave(n, 0)
+            interleave(n, 1)
+            quant(n, 0)
+            quant(n, 1)
+
+        def score_pass(bank, b, s, part, start, stop):
+            q = "q%s%d" % (part, b)
+            k = "k%s%d" % (part, b)
+            nc.tensor.matmul_mx(
+                out=bank[:],
+                lhsT=codes[q][:, 128 * s : 128 * (s + 1)].bitcast(FP8X4),
+                lhsT_scale=scales[q][:, 128 * s : 128 * (s + 1)],
+                rhs=codes[k][:].bitcast(FP8X4),
+                rhs_scale=scales[k][:],
+                start=start,
+                stop=stop,
+            )
+
+        def score_out(bank, b, s, engine):
+            o = result[b][:, s, :].rearrange("p (m j) -> p m j", j=4)
+            i = bank[:].rearrange("p (j m) -> p m j", j=4)
+            if engine == "scalar":
+                nc.scalar.copy(out=o, in_=i)
+            else:
+                nc.vector.tensor_copy(out=o, in_=i)
+            nc.sync.dma_start(out=out[b].rearrange("(m s) k -> m s k", s=4)[:, s, :], in_=result[b][:, s, :])
+
+        with tc.manual_schedule():
+            nc.sync.dma_start(out=scale_col[:], in_=x_re_scale.rearrange("a b (p j) -> (a b p) j", j=4))
+            make_identity(nc, ident[:])
+            load("xi0", 2)
+            load_bytes(0)
+            load("wqr", 2)
+            load("wqi")
+            load_bytes(1)
+            load("wkr")
+            load("wki")
+            load("xi1")
+            for n in bias_in:
+                nc.sync.dma_start(out=bias[n][:], in_=bias_in[n].rearrange("(p t) -> p t", t=4))
+
+            nc.vector.memset(dummy[:], 0.0)
+            nc.scalar.activation(out=dummy[:], in_=dummy[:], func=ACT.Identity, bias=0.0, scale=1.0)
+
+            bank = bank_tile()
+            for j in range(4):
+                nc.tensor.transpose(bank[:, 128 * j : 128 * (j + 1)], scale_col[:, j : j + 1].to_broadcast([P, P]), ident[:])
+            nc.scalar.copy(out=scale_row[:].rearrange("p (n j) -> p n j", j=4), in_=bank[:].rearrange("p (j n) -> p n j", j=4))
+
+            for b in range(BATCHES):
+                for s in range(4):
+                    widen(b, s)
+            for n in ("xi0", "wqr", "xr0", "wqi", "wkr", "wki"):
+                turn(n)
+                quant(n)
+            turn("xi1")
+            negate(0)
+            negate(1)
+            quant("xn0")
+            quant("xi1")
+            turn("xr1", (1,))
+            quant("xr1")
+            unit("q", "i", 0)
+            pack("qi0")
+            unit("k", "i", 0)
+            pack("ki0")
+            unit("q", "r", 0)
+            pack("qr0")
+            quant("xn1")
+            unit("k", "r", 0)
+            pack("kr0")
+            unit("q", "i", 1)
+            pack("qi1")
+            unit("k", "i", 1)
+            pack("ki1")
+            unit("k", "r", 1)
+            pack("kr1")
+            unit("q", "r", 1)
+            pack("qr1")
+            for b, group in ((0, 1), (1, 2)):
+                for first in range(0, 4, group):
+                    banks = {s: bank_tile() for s in range(first, first + group)}
+                    for s in banks:
+                        score_pass(banks[s], b, s, "i", True, False)
+                    for s in banks:
+                        score_pass(banks[s], b, s, "r", False, True)
+                        score_out(banks[s], b, s, "vector" if b == 1 and s % 2 == 1 else "scalar")

@@ -36,194 +36,261 @@ def tile_teleportationattention_pa_kernel(
         ident = new("ident", [P, P], F32)
         dummy = new("dummy", [P, 1], F32)
         scale_col = new("scale_col", [P, 4], F32)
-        scale_row = new("scale_row", [P, K], F32)
         bias_in = {"qr": bq_re, "qi": bq_im, "kr": bk_re, "ki": bk_im}
         bias = {}
         for n in bias_in:
             bias[n] = new("bias_" + n, [P, 4], BF16)
 
+        inputs = ("wqr", "wqi", "wkr", "wki", "xr0", "xi0", "xr1", "xi1")
+        halved = ("xi0", "wqr", "wqi", "wkr", "wki", "xi1", "xr0", "xr1")
         raw = {}
-        for n in ("wqr", "wqi", "wkr", "wki", "xr0", "xi0", "xr1", "xi1"):
-            raw[n] = new("raw_" + n, [P, 4, K], BF16)
-        xbytes = [new("xbytes%d" % b, [P, 4, K], U8) for b in range(BATCHES)]
+        for n in inputs:
+            if n in halved:
+                raw[n] = [new("raw_%s_%d" % (n, h), [P, 2, K], BF16)[:] for h in range(2)]
+            else:
+                whole = new("raw_" + n, [P, 4, K], BF16)
+                raw[n] = [whole[:, 2 * h : 2 * h + 2, :] for h in range(2)]
+                raw[n].append(whole[:])
+        xbytes = [[new("xbytes%d_%d" % (b, h), [P, 2 * K], U8) for h in range(2)] for b in range(BATCHES)]
+        projected = ("qr0", "qi0", "kr0", "ki0", "qr1", "qi1", "kr1", "ki1")
         grouped = {}
         codes = {}
         scales = {}
-        for n in ("wqr", "wqi", "wkr", "wki", "xr0", "xi0", "xn0", "xr1", "xi1", "xn1", "qr0", "qi0", "kr0", "ki0", "qr1", "qi1", "kr1", "ki1"):
+        for n in inputs + ("xn0", "xn1") + projected:
             grouped[n] = new("grp_" + n, [P, 4 * 512], BF16)
             codes[n] = new("codes_" + n, [P, 512], U32)
             scales[n] = new("scales_" + n, [P, 512], U8)
         planes = {}
-        for n in ("qr0", "qi0", "kr0", "ki0", "qr1", "qi1", "kr1", "ki1"):
+        for n in projected:
             planes[n] = new("planes_" + n, [P, 4, 512], BF16)
-        result = [new("result%d" % b, [P, 4, 512], F32) for b in range(BATCHES)]
+        result = [[new("result%d_%d" % (b, s), [P, 512], F32) for s in range(4)] for b in range(BATCHES)]
 
-        w_view = {"wqr": Wq_re, "wqi": Wq_im, "wkr": Wk_re, "wki": Wk_im}
-        src = {}
-        for n in w_view:
-            src[n] = w_view[n].rearrange("(m s) k -> m s k", s=4)
-        for b in range(BATCHES):
-            src["xi%d" % b] = x_im[b].rearrange("(m s) k -> m s k", s=4)
+        src = {"wqr": Wq_re, "wqi": Wq_im, "wkr": Wk_re, "wki": Wk_im, "xi0": x_im[0], "xi1": x_im[1]}
 
-        def load(n, parts=1):
-            step = 4 // parts
-            for i in range(parts):
-                nc.sync.dma_start(out=raw[n][:, i * step : (i + 1) * step, :], in_=src[n][:, i * step : (i + 1) * step, :])
+        def load(n, h=None):
+            rows = src[n].rearrange("(m s) k -> m s k", s=4)
+            if h is None:
+                nc.sync.dma_start(out=raw[n][2], in_=rows)
+            else:
+                nc.sync.dma_start(out=raw[n][h], in_=rows[:, 2 * h : 2 * h + 2, :])
 
-        def load_bytes(b):
-            nc.sync.dma_start(out=xbytes[b][:], in_=x_re_bytes[b].rearrange("(m s) k -> m s k", s=4))
+        def load_bytes(b, h):
+            nc.sync.dma_start(out=xbytes[b][h][:], in_=x_re_bytes[b].rearrange("(m h c) k -> m h (c k)", h=2, c=2)[:, h, :])
 
-        def widen(b, s):
+        def load_bias(n):
+            nc.sync.dma_start(out=bias[n][:], in_=bias_in[n].rearrange("(p t) -> p t", t=4))
+
+        def widen(b, h, engine="vector"):
+            source = xbytes[b][h][:].bitcast(FP8)
+            target = raw["xr%d" % b][h].rearrange("p c k -> p (c k)")
+            if engine == "scalar":
+                nc.scalar.copy(out=target, in_=source)
+            else:
+                nc.vector.tensor_copy(out=target, in_=source)
+
+        turned = {}
+
+        def turn(n, h):
+            bank = bank_tile()
+            turned[n, h] = bank
+            v = bank[:].rearrange("p (u c r) -> p u c r", c=2, u=2)
+            for c in range(2):
+                words = raw[n][h][:, c, :].bitcast(F32)
+                for u in range(2):
+                    nc.tensor.transpose(v[:, u, c, :], words[:, u:256:2], ident[:])
+
+        def gather(n, h, engine="scalar"):
+            target = grouped[n][:, 1024 * h : 1024 * (h + 1)].bitcast(F32).rearrange("p (r u) -> p r u", u=2)
+            source = turned[n, h][:].rearrange("p (u r) -> p r u", u=2)
+            if engine == "scalar":
+                nc.scalar.copy(out=target, in_=source)
+            else:
+                nc.vector.tensor_copy(out=target, in_=source)
+
+        def gather_scaled(n, h):
             nc.vector.tensor_tensor(
-                out=raw["xr%d" % b][:, s, :], in0=xbytes[b][:, s, :].bitcast(FP8), in1=scale_row[:], op=ALU.mult
+                out=grouped[n][:, 1024 * h : 1024 * (h + 1)].rearrange("p (r u e) -> p r u e", u=2, e=2),
+                in0=turned[n, h][:].bitcast(BF16).rearrange("p (u r e) -> p r u e", u=2, e=2),
+                in1=scale_col[:].rearrange("p (u e) -> p u e", e=2).unsqueeze(1).to_broadcast([P, 256, 2, 2]),
+                op=ALU.mult,
             )
 
-        def turn(n, on_vector=()):
-            for h in range(2):
-                bank = bank_tile()
-                v = bank[:].rearrange("p (c u r) -> p c u r", c=2, u=2)
-                for c in range(2):
-                    words = raw[n][:, 2 * h + c, :].bitcast(F32)
-                    for u in range(2):
-                        nc.tensor.transpose(v[:, c, u, :], words[:, u:256:2], ident[:])
-                target = grouped[n][:, 1024 * h : 1024 * (h + 1)].bitcast(F32).rearrange("p (c r u) -> p c r u", c=2, u=2)
-                if h in on_vector:
-                    nc.vector.tensor_copy(out=target, in_=v.rearrange("p c u r -> p c r u"))
-                else:
-                    nc.scalar.copy(out=target, in_=v.rearrange("p c u r -> p c r u"))
-
-        def quant(n, h=None):
-            lo, hi = (0, 512) if h is None else (256 * h, 256 * (h + 1))
+        def quant(n, lo=0, hi=4):
             nc.vector.quantize_mx(
-                out=codes[n][:, lo:hi].bitcast(FP8X4), scales=scales[n][:, lo:hi], in_=grouped[n][:, 4 * lo : 4 * hi]
+                out=codes[n][:, P * lo : P * hi].bitcast(FP8X4),
+                scales=scales[n][:, P * lo : P * hi],
+                in_=grouped[n][:, 4 * P * lo : 4 * P * hi],
             )
 
         def negate(b):
             nc.vector.tensor_scalar(out=grouped["xn%d" % b][:], in0=grouped["xi%d" % b][:], scalar1=-1.0, scalar2=None, op0=ALU.mult)
 
-        def mm(bank, w, t, x, start, stop):
+        def mm(target, w, t, x, lo, hi, start, stop):
             nc.tensor.matmul_mx(
-                out=bank[:],
-                lhsT=codes[w][:, 128 * t : 128 * (t + 1)].bitcast(FP8X4),
-                lhsT_scale=scales[w][:, 128 * t : 128 * (t + 1)],
-                rhs=codes[x][:].bitcast(FP8X4),
-                rhs_scale=scales[x][:],
+                out=target,
+                lhsT=codes[w][:, P * t : P * (t + 1)].bitcast(FP8X4),
+                lhsT_scale=scales[w][:, P * t : P * (t + 1)],
+                rhs=codes[x][:, P * lo : P * hi].bitcast(FP8X4),
+                rhs_scale=scales[x][:, P * lo : P * hi],
                 start=start,
                 stop=stop,
             )
 
-        def operands(side, part, b):
+        def operands(n):
+            side, part, b = n
             if part == "r":
-                return [("w%sr" % side, "xr%d" % b), ("w%si" % side, "xn%d" % b)]
-            return [("w%sr" % side, "xi%d" % b), ("w%si" % side, "xr%d" % b)]
+                return [("w%sr" % side, "xr" + b), ("w%si" % side, "xn" + b)]
+            return [("w%sr" % side, "xi" + b), ("w%si" % side, "xr" + b)]
 
-        def leave(bank, side, part, b, t, engine):
-            plane = planes["%s%s%d" % (side, part, b)][:, t, :]
-            column = bias[side + part][:, t : t + 1]
+        summed = {}
+
+        def project(n, t):
+            bank = bank_tile()
+            summed[n, t] = bank
+            for i, (w, x) in enumerate(operands(n)):
+                mm(bank[:], w, t, x, 0, 4, i == 0, i == 1)
+
+        def leave(n, t, engine="scalar"):
+            plane = planes[n][:, t, :]
+            column = bias[n[:2]][:, t : t + 1]
             if engine == "scalar":
-                nc.scalar.activation(out=plane, in_=bank[:], func=ACT.Identity, bias=column, scale=1.0)
+                nc.scalar.activation(out=plane, in_=summed[n, t][:], func=ACT.Identity, bias=column, scale=1.0)
             else:
-                nc.vector.tensor_scalar(out=plane, in0=bank[:], scalar1=column, scalar2=None, op0=ALU.add)
+                nc.vector.tensor_scalar(out=plane, in0=summed[n, t][:], scalar1=column, scalar2=None, op0=ALU.add)
 
-        def unit(side, part, b, on_vector=()):
-            ops = operands(side, part, b)
+        def unit(n, on_vector=()):
             for t in range(4):
-                bank = bank_tile()
-                for i in range(2):
-                    mm(bank, ops[i][0], t, ops[i][1], i == 0, i == 1)
-                leave(bank, side, part, b, t, "vector" if t in on_vector else "scalar")
+                project(n, t)
+                leave(n, t, "vector" if t in on_vector else "scalar")
 
-        def interleave(n, h):
-            nc.vector.tensor_copy(
-                out=grouped[n][:, 1024 * h : 1024 * (h + 1)].rearrange("p (c i t) -> p c t i", i=4, t=4),
-                in_=planes[n][:, :, 256 * h : 256 * (h + 1)].rearrange("p t (c i) -> p c t i", i=4),
+        def project_slot(n, s):
+            bank = bank_tile()
+            summed[n, s] = bank
+            for t in range(4):
+                for i, (w, x) in enumerate(operands(n)):
+                    mm(bank[:, P * t : P * (t + 1)], w, t, x, s, s + 1, i == 0, i == 1)
+
+        def leave_slot(n, s):
+            nc.vector.tensor_tensor(
+                out=grouped[n][:, 512 * s : 512 * (s + 1)].rearrange("p (r t) -> p r t", t=4),
+                in0=summed[n, s][:].rearrange("p (t r) -> p r t", t=4),
+                in1=bias[n[:2]][:].unsqueeze(1).to_broadcast([P, P, 4]),
+                op=ALU.add,
             )
+
+        def interleave(n, h, engine="vector"):
+            target = grouped[n][:, 1024 * h : 1024 * (h + 1)].rearrange("p (c i t) -> p c t i", i=4, t=4)
+            source = planes[n][:, :, 256 * h : 256 * (h + 1)].rearrange("p t (c i) -> p c t i", i=4)
+            if engine == "scalar":
+                nc.scalar.copy(out=target, in_=source)
+            else:
+                nc.vector.tensor_copy(out=target, in_=source)
 
         def pack(n):
             interleave(n, 0)
             interleave(n, 1)
-            quant(n, 0)
-            quant(n, 1)
+            quant(n, 0, 2)
+            quant(n, 2, 4)
 
-        def score_pass(bank, b, s, part, start, stop):
-            q = "q%s%d" % (part, b)
-            k = "k%s%d" % (part, b)
-            nc.tensor.matmul_mx(
-                out=bank[:],
-                lhsT=codes[q][:, 128 * s : 128 * (s + 1)].bitcast(FP8X4),
-                lhsT_scale=scales[q][:, 128 * s : 128 * (s + 1)],
-                rhs=codes[k][:].bitcast(FP8X4),
-                rhs_scale=scales[k][:],
-                start=start,
-                stop=stop,
-            )
+        scored = {}
 
-        def score_out(bank, b, s, engine):
-            o = result[b][:, s, :].rearrange("p (m j) -> p m j", j=4)
-            i = bank[:].rearrange("p (j m) -> p m j", j=4)
+        def score(b, s, part, start):
+            if start:
+                scored[b, s] = bank_tile()
+            mm(scored[b, s][:], "q%s%d" % (part, b), s, "k%s%d" % (part, b), 0, 4, start, not start)
+
+        def store(b, s, engine="scalar"):
+            o = result[b][s][:].rearrange("p (m j) -> p m j", j=4)
+            i = scored[b, s][:].rearrange("p (j m) -> p m j", j=4)
             if engine == "scalar":
                 nc.scalar.copy(out=o, in_=i)
             else:
                 nc.vector.tensor_copy(out=o, in_=i)
-            nc.sync.dma_start(out=out[b].rearrange("(m s) k -> m s k", s=4)[:, s, :], in_=result[b][:, s, :])
+            nc.sync.dma_start(out=out[b].rearrange("(m s) k -> m s k", s=4)[:, s, :], in_=result[b][s][:])
 
         with tc.manual_schedule():
-            nc.sync.dma_start(out=scale_col[:], in_=x_re_scale.rearrange("a b (p j) -> (a b p) j", j=4))
+            load_bytes(0, 0)
             make_identity(nc, ident[:])
-            load("xi0", 2)
-            load_bytes(0)
-            load("wqr", 2)
-            load("wqi")
-            load_bytes(1)
-            load("wkr")
-            load("wki")
-            load("xi1")
-            for n in bias_in:
-                nc.sync.dma_start(out=bias[n][:], in_=bias_in[n].rearrange("(p t) -> p t", t=4))
-
+            load("xi0", 0)
+            load_bytes(0, 1)
+            load("xi0", 1)
+            nc.sync.dma_start(out=scale_col[:], in_=x_re_scale.rearrange("a b (p j) -> (a b p) j", j=4))
+            load("wqr", 0)
+            load("wqr", 1)
+            load_bytes(1, 0)
+            load_bytes(1, 1)
+            for n in ("wqi", "wkr", "wki", "xi1"):
+                load(n, 0)
+                load(n, 1)
+            for n in ("qi", "ki", "qr", "kr"):
+                load_bias(n)
             nc.vector.memset(dummy[:], 0.0)
             nc.scalar.activation(out=dummy[:], in_=dummy[:], func=ACT.Identity, bias=0.0, scale=1.0)
 
-            bank = bank_tile()
-            for j in range(4):
-                nc.tensor.transpose(bank[:, 128 * j : 128 * (j + 1)], scale_col[:, j : j + 1].to_broadcast([P, P]), ident[:])
-            nc.scalar.copy(out=scale_row[:].rearrange("p (n j) -> p n j", j=4), in_=bank[:].rearrange("p (j n) -> p n j", j=4))
-
-            for b in range(BATCHES):
-                for s in range(4):
-                    widen(b, s)
-            for n in ("xi0", "wqr", "xr0", "wqi", "wkr", "wki"):
-                turn(n)
-                quant(n)
-            turn("xi1")
+            widen(0, 0)
+            widen(0, 1)
+            for h in range(2):
+                turn("xi0", h)
+                gather("xi0", h)
+                turn("xr0", h)
+                gather_scaled("xr0", h)
+            for h in range(2):
+                turn("wqr", h)
+                gather("wqr", h)
+            widen(1, 0, "vector")
+            widen(1, 1, "vector")
+            quant("xi0")
+            quant("xr0")
+            for h in range(2):
+                turn("wqi", h)
+                gather("wqi", h)
+            quant("wqr")
+            for h in range(2):
+                turn("xr1", h)
+                gather_scaled("xr1", h)
+            quant("wqi")
+            for n in ("wkr", "wki", "xi1"):
+                for h in range(2):
+                    turn(n, h)
+                    gather(n, h)
             negate(0)
-            negate(1)
+            quant("wkr")
+            quant("wki")
             quant("xn0")
-            quant("xi1")
-            turn("xr1", (1,))
             quant("xr1")
-            unit("q", "i", 0)
+            quant("xi1")
+            unit("qi0")
+            negate(1)
             pack("qi0")
-            unit("k", "i", 0)
-            pack("ki0")
-            unit("q", "r", 0)
-            pack("qr0")
             quant("xn1")
-            unit("k", "r", 0)
+            unit("ki0")
+            pack("ki0")
+            unit("qr0")
+            pack("qr0")
+            unit("kr0")
+
+            unit("ki1")
             pack("kr0")
-            unit("q", "i", 1)
-            pack("qi1")
-            unit("k", "i", 1)
+            project("kr1", 0)
+            leave("kr1", 0, "vector")
+            for t in range(1, 4):
+                project("kr1", t)
+                leave("kr1", t)
             pack("ki1")
-            unit("k", "r", 1)
+            unit("qi1")
             pack("kr1")
-            unit("q", "r", 1)
-            pack("qr1")
-            for b, group in ((0, 1), (1, 2)):
-                for first in range(0, 4, group):
-                    banks = {s: bank_tile() for s in range(first, first + group)}
-                    for s in banks:
-                        score_pass(banks[s], b, s, "i", True, False)
-                    for s in banks:
-                        score_pass(banks[s], b, s, "r", False, True)
-                        score_out(banks[s], b, s, "vector" if b == 1 and s % 2 == 1 else "scalar")
+            for s in range(4):
+                score(0, s, "i", True)
+                score(0, s, "r", False)
+                store(0, s)
+            pack("qi1")
+            for s in range(4):
+                project_slot("qr1", s)
+                leave_slot("qr1", s)
+                if s > 0:
+                    quant("qr1", s - 1, s)
+            quant("qr1", 3, 4)
+            for s in range(4):
+                score(1, s, "i", True)
+                score(1, s, "r", False)
+                store(1, s, "vector" if s == 3 else "scalar")

@@ -35,6 +35,7 @@ def tile_teleportationattention_pa_kernel(
 
         ident = new("ident", [P, P], F32)
         dummy = new("dummy", [P, 1], F32)
+        one = new("one", [P, 1], F32)
         scale_col = new("scale_col", [P, 4], F32)
         bias_in = {"qr": bq_re, "qi": bq_im, "kr": bk_re, "ki": bk_im}
         bias = {}
@@ -88,7 +89,23 @@ def tile_teleportationattention_pa_kernel(
             else:
                 nc.vector.tensor_copy(out=target, in_=source)
 
+        def widen_sorted(b, h):
+            nc.vector.tensor_scalar(
+                out=raw["xr%d" % b][h].rearrange("p c k -> p (c k)").rearrange("p (u w e) -> p w u e", u=2, e=2),
+                in0=xbytes[b][h][:].bitcast(FP8).rearrange("p (w u e) -> p w u e", u=2, e=2),
+                scalar1=one[:],
+                scalar2=None,
+                op0=ALU.mult,
+            )
+
         turned = {}
+
+        def turn_sorted(n, h):
+            bank = bank_tile()
+            turned[n, h] = bank
+            words = raw[n][h].rearrange("p c k -> p (c k)").bitcast(F32)
+            for j in range(4):
+                nc.tensor.transpose(bank[:, P * j : P * (j + 1)], words[:, P * j : P * (j + 1)], ident[:])
 
         def turn(n, h):
             bank = bank_tile()
@@ -186,6 +203,12 @@ def tile_teleportationattention_pa_kernel(
             else:
                 nc.vector.tensor_copy(out=target, in_=source)
 
+        def interleave_whole(n):
+            nc.vector.tensor_copy(
+                out=grouped[n][:].rearrange("p (c i t) -> p c t i", i=4, t=4),
+                in_=planes[n][:].rearrange("p t (c i) -> p c t i", i=4),
+            )
+
         def pack(n):
             interleave(n, 0)
             interleave(n, 1)
@@ -215,11 +238,12 @@ def tile_teleportationattention_pa_kernel(
             load_bytes(0, 1)
             load("xi0", 1)
             nc.sync.dma_start(out=scale_col[:], in_=x_re_scale.rearrange("a b (p j) -> (a b p) j", j=4))
-            load("wqr", 0)
-            load("wqr", 1)
+            for n in ("wqr", "wqi"):
+                load(n, 0)
+                load(n, 1)
             load_bytes(1, 0)
             load_bytes(1, 1)
-            for n in ("wqi", "wkr", "wki", "xi1"):
+            for n in ("wkr", "wki", "xi1"):
                 load(n, 0)
                 load(n, 1)
             for n in ("qi", "ki", "qr", "kr"):
@@ -227,58 +251,52 @@ def tile_teleportationattention_pa_kernel(
             nc.vector.memset(dummy[:], 0.0)
             nc.scalar.activation(out=dummy[:], in_=dummy[:], func=ACT.Identity, bias=0.0, scale=1.0)
 
-            widen(0, 0)
-            widen(0, 1)
+            nc.vector.memset(one[:], 1.0)
+
+            widen_sorted(0, 0)
+            widen_sorted(0, 1)
             for h in range(2):
                 turn("xi0", h)
                 gather("xi0", h)
-                turn("xr0", h)
+                turn_sorted("xr0", h)
                 gather_scaled("xr0", h)
-            for h in range(2):
-                turn("wqr", h)
-                gather("wqr", h)
-            widen(1, 0, "vector")
-            widen(1, 1, "vector")
+            for n in ("wqr", "wqi"):
+                for h in range(2):
+                    turn(n, h)
+                    gather(n, h)
             quant("xi0")
             quant("xr0")
-            for h in range(2):
-                turn("wqi", h)
-                gather("wqi", h)
+            widen_sorted(1, 0)
+            widen_sorted(1, 1)
             quant("wqr")
-            for h in range(2):
-                turn("xr1", h)
-                gather_scaled("xr1", h)
             quant("wqi")
-            for n in ("wkr", "wki", "xi1"):
+            for n in ("wkr", "wki"):
                 for h in range(2):
                     turn(n, h)
                     gather(n, h)
             negate(0)
             quant("wkr")
-            quant("wki")
             quant("xn0")
-            quant("xr1")
+            for h in range(2):
+                turn_sorted("xr1", h)
+            quant("wki")
+            for h in range(2):
+                gather_scaled("xr1", h)
+            for h in range(2):
+                turn("xi1", h)
+                gather("xi1", h)
             quant("xi1")
-            unit("qi0")
             negate(1)
-            pack("qi0")
+            quant("xr1")
             quant("xn1")
-            unit("ki0")
-            pack("ki0")
-            unit("qr0")
-            pack("qr0")
-            unit("kr0")
-
-            unit("ki1")
-            pack("kr0")
-            project("kr1", 0)
-            leave("kr1", 0, "vector")
-            for t in range(1, 4):
-                project("kr1", t)
-                leave("kr1", t)
-            pack("ki1")
+            order = ("qi0", "ki0", "qr0", "kr0", "ki1", "kr1")
+            for i, n in enumerate(order):
+                unit(n)
+                interleave_whole(n)
+                if i > 0:
+                    quant(order[i - 1])
             unit("qi1")
-            pack("kr1")
+            quant("kr1")
             for s in range(4):
                 score(0, s, "i", True)
                 score(0, s, "r", False)

@@ -35,7 +35,6 @@ def tile_teleportationattention_pa_kernel(
 
         ident = new("ident", [P, P], F32)
         dummy = new("dummy", [P, 1], F32)
-        one = new("one", [P, 1], F32)
         scale_col = new("scale_col", [P, 4], F32)
         bias_in = {"qr": bq_re, "qi": bq_im, "kr": bk_re, "ki": bk_im}
         bias = {}
@@ -89,23 +88,7 @@ def tile_teleportationattention_pa_kernel(
             else:
                 nc.vector.tensor_copy(out=target, in_=source)
 
-        def widen_sorted(b, h):
-            nc.vector.tensor_scalar(
-                out=raw["xr%d" % b][h].rearrange("p c k -> p (c k)").rearrange("p (u w e) -> p w u e", u=2, e=2),
-                in0=xbytes[b][h][:].bitcast(FP8).rearrange("p (w u e) -> p w u e", u=2, e=2),
-                scalar1=one[:],
-                scalar2=None,
-                op0=ALU.mult,
-            )
-
         turned = {}
-
-        def turn_sorted(n, h):
-            bank = bank_tile()
-            turned[n, h] = bank
-            words = raw[n][h].rearrange("p c k -> p (c k)").bitcast(F32)
-            for j in range(4):
-                nc.tensor.transpose(bank[:, P * j : P * (j + 1)], words[:, P * j : P * (j + 1)], ident[:])
 
         def turn(n, h):
             bank = bank_tile()
@@ -251,14 +234,13 @@ def tile_teleportationattention_pa_kernel(
             nc.vector.memset(dummy[:], 0.0)
             nc.scalar.activation(out=dummy[:], in_=dummy[:], func=ACT.Identity, bias=0.0, scale=1.0)
 
-            nc.vector.memset(one[:], 1.0)
 
-            widen_sorted(0, 0)
-            widen_sorted(0, 1)
+            widen(0, 0)
+            widen(0, 1)
             for h in range(2):
                 turn("xi0", h)
                 gather("xi0", h)
-                turn_sorted("xr0", h)
+                turn("xr0", h)
                 gather_scaled("xr0", h)
             for n in ("wqr", "wqi"):
                 for h in range(2):
@@ -266,8 +248,8 @@ def tile_teleportationattention_pa_kernel(
                     gather(n, h)
             quant("xi0")
             quant("xr0")
-            widen_sorted(1, 0)
-            widen_sorted(1, 1)
+            widen(1, 0)
+            widen(1, 1)
             quant("wqr")
             quant("wqi")
             for n in ("wkr", "wki"):
@@ -278,7 +260,7 @@ def tile_teleportationattention_pa_kernel(
             quant("wkr")
             quant("xn0")
             for h in range(2):
-                turn_sorted("xr1", h)
+                turn("xr1", h)
             quant("wki")
             for h in range(2):
                 gather_scaled("xr1", h)

@@ -28,7 +28,7 @@ def tile_teleportationattention_pa_kernel(
         psum = ctx.enter_context(tc.psum_pool(name="psum", bufs=8))
 
         def new(name, shape, dtype):
-            return keep.tile(shape, dtype, name=name, align_bytes=64)
+            return keep.tile(shape, dtype, name=name, align_bytes=256)
 
         def bank_tile():
             return psum.tile([P, 512], F32, name="bank")
@@ -51,7 +51,7 @@ def tile_teleportationattention_pa_kernel(
                 whole = new("raw_" + n, [P, 4, K], BF16)
                 raw[n] = [whole[:, 2 * h : 2 * h + 2, :] for h in range(2)]
                 raw[n].append(whole[:])
-        xbytes = [[new("xbytes%d_%d" % (b, h), [P, 2 * K], U8) for h in range(2)] for b in range(BATCHES)]
+        xbytes = [new("xbytes%d" % b, [P, 4 * K], U8) for b in range(BATCHES)]
         projected = ("qr0", "qi0", "kr0", "ki0", "qr1", "qi1", "kr1", "ki1")
         grouped = {}
         codes = {}
@@ -74,14 +74,17 @@ def tile_teleportationattention_pa_kernel(
             else:
                 nc.sync.dma_start(out=raw[n][h], in_=rows[:, 2 * h : 2 * h + 2, :])
 
-        def load_bytes(b, h):
-            nc.sync.dma_start(out=xbytes[b][h][:], in_=x_re_bytes[b].rearrange("(m h c) k -> m h (c k)", h=2, c=2)[:, h, :])
+        def load_bytes(b, lo=0, hi=4):
+            nc.sync.dma_start(out=xbytes[b][:, K * lo : K * hi], in_=x_re_bytes[b].rearrange("(m s) k -> m (s k)", s=4)[:, K * lo : K * hi])
+
+        def load_scale(queue):
+            queue.dma_start(out=scale_col[:], in_=x_re_scale.rearrange("a b (p j) -> (a b p) j", j=4))
 
         def load_bias(n):
             nc.sync.dma_start(out=bias[n][:], in_=bias_in[n].rearrange("(p t) -> p t", t=4))
 
         def widen(b, h, engine="vector"):
-            source = xbytes[b][h][:].bitcast(FP8)
+            source = xbytes[b][:, 2 * K * h : 2 * K * (h + 1)].bitcast(FP8)
             target = raw["xr%d" % b][h].rearrange("p c k -> p (c k)")
             if engine == "scalar":
                 nc.scalar.copy(out=target, in_=source)
@@ -215,61 +218,71 @@ def tile_teleportationattention_pa_kernel(
             nc.sync.dma_start(out=out[b].rearrange("(m s) k -> m s k", s=4)[:, s, :], in_=result[b][s][:])
 
         with tc.manual_schedule():
-            load_bytes(0, 0)
+            load_scale(nc.scalar)
             make_identity(nc, ident[:])
+            load_bytes(0, 0, 2)
             load("xi0", 0)
-            load_bytes(0, 1)
+            load_bytes(0, 2, 4)
+            load_bytes(1, 0, 2)
             load("xi0", 1)
-            nc.sync.dma_start(out=scale_col[:], in_=x_re_scale.rearrange("a b (p j) -> (a b p) j", j=4))
-            for n in ("wqr", "wqi"):
-                load(n, 0)
-                load(n, 1)
-            load_bytes(1, 0)
-            load_bytes(1, 1)
-            for n in ("wkr", "wki", "xi1"):
-                load(n, 0)
-                load(n, 1)
-            for n in ("qi", "ki", "qr", "kr"):
-                load_bias(n)
+            load("wqr", 0)
+            load_bytes(1, 2, 4)
+            load("wqr", 1)
+            load("wqi", 0)
+            load("wqi", 1)
+            load("wkr", 0)
+            load("wkr", 1)
+            load("wki", 0)
+            load("wki", 1)
+            load("xi1", 0)
+            load("xi1", 1)
+            load_bias("qi")
+            load_bias("ki")
+            load_bias("qr")
+            load_bias("kr")
             nc.vector.memset(dummy[:], 0.0)
             nc.scalar.activation(out=dummy[:], in_=dummy[:], func=ACT.Identity, bias=0.0, scale=1.0)
 
-
             widen(0, 0)
             widen(0, 1)
+            widen(1, 0)
             for h in range(2):
                 turn("xi0", h)
                 gather("xi0", h)
                 turn("xr0", h)
                 gather_scaled("xr0", h)
-            for n in ("wqr", "wqi"):
-                for h in range(2):
-                    turn(n, h)
-                    gather(n, h)
+            widen(1, 1)
+            turn("wqr", 0)
+            gather("wqr", 0)
+            turn("xr1", 0)
+            turn("wqr", 1)
+            gather("wqr", 1)
             quant("xi0")
             quant("xr0")
-            widen(1, 0)
-            widen(1, 1)
+            turn("wqi", 0)
+            gather("wqi", 0)
+            gather_scaled("xr1", 0)
+            turn("wqi", 1)
+            gather("wqi", 1)
             quant("wqr")
+            turn("wkr", 0)
+            gather("wkr", 0)
+            turn("xr1", 1)
             quant("wqi")
-            for n in ("wkr", "wki"):
+            gather_scaled("xr1", 1)
+            turn("wkr", 1)
+            gather("wkr", 1)
+            for n in ("wki", "xi1"):
                 for h in range(2):
                     turn(n, h)
                     gather(n, h)
             negate(0)
             quant("wkr")
-            quant("xn0")
-            for h in range(2):
-                turn("xr1", h)
             quant("wki")
-            for h in range(2):
-                gather_scaled("xr1", h)
-            for h in range(2):
-                turn("xi1", h)
-                gather("xi1", h)
-            quant("xi1")
-            negate(1)
+            quant("xn0")
             quant("xr1")
+            negate(1)
+            quant("xi1")
             quant("xn1")
             order = ("qi0", "ki0", "qr0", "kr0", "ki1", "kr1")
             for i, n in enumerate(order):

@@ -17,6 +17,8 @@ ACT = mybir.ActivationFunctionType
 P = 128
 K = 512
 BATCHES = 2
+SORTED = ()
+WHOLE = ()
 
 
 def tile_teleportationattention_pa_kernel(
@@ -25,16 +27,17 @@ def tile_teleportationattention_pa_kernel(
     nc = tc.nc
     with ExitStack() as ctx:
         keep = ctx.enter_context(tc.tile_pool(name="keep", bufs=1))
-        psum = ctx.enter_context(tc.psum_pool(name="psum", bufs=8))
+        psum = ctx.enter_context(tc.psum_pool(name="psum", bufs=1))
 
         def new(name, shape, dtype):
             return keep.tile(shape, dtype, name=name, align_bytes=256)
 
-        def bank_tile():
-            return psum.tile([P, 512], F32, name="bank")
+        def bank_tile(j):
+            return psum.tile([P, 512], F32, name="bank%d" % j)
 
         ident = new("ident", [P, P], F32)
-        dummy = new("dummy", [P, 1], F32)
+        idle = new("idle", [P, 512], BF16)
+        one = new("one", [P, 1], F32)
         scale_col = new("scale_col", [P, 4], F32)
         bias_in = {"qr": bq_re, "qi": bq_im, "kr": bk_re, "ki": bk_im}
         bias = {}
@@ -42,16 +45,18 @@ def tile_teleportationattention_pa_kernel(
             bias[n] = new("bias_" + n, [P, 4], BF16)
 
         inputs = ("wqr", "wqi", "wkr", "wki", "xr0", "xi0", "xr1", "xi1")
-        halved = ("xi0", "wqr", "wqi", "wkr", "wki", "xi1", "xr0", "xr1")
         raw = {}
+        ordered = {}
+        whole = {}
         for n in inputs:
-            if n in halved:
-                raw[n] = [new("raw_%s_%d" % (n, h), [P, 2, K], BF16)[:] for h in range(2)]
+            if n in WHOLE:
+                whole[n] = new("raw_" + n, [P, 4 * K], BF16)
+                raw[n] = [whole[n][:, 2 * K * h : 2 * K * (h + 1)] for h in range(2)]
             else:
-                whole = new("raw_" + n, [P, 4, K], BF16)
-                raw[n] = [whole[:, 2 * h : 2 * h + 2, :] for h in range(2)]
-                raw[n].append(whole[:])
-        xbytes = [new("xbytes%d" % b, [P, 4 * K], U8) for b in range(BATCHES)]
+                raw[n] = [new("raw_%s_%d" % (n, h), [P, 2 * K], BF16)[:] for h in range(2)]
+        for n in SORTED:
+            ordered[n] = [new("ord_%s_%d" % (n, h), [P, 2 * K], BF16) for h in range(2)]
+        xbytes = [[new("xbytes%d_%d" % (b, h), [P, 2 * K], U8) for h in range(2)] for b in range(BATCHES)]
         projected = ("qr0", "qi0", "kr0", "ki0", "qr1", "qi1", "kr1", "ki1")
         grouped = {}
         codes = {}
@@ -67,25 +72,35 @@ def tile_teleportationattention_pa_kernel(
 
         src = {"wqr": Wq_re, "wqi": Wq_im, "wkr": Wk_re, "wki": Wk_im, "xi0": x_im[0], "xi1": x_im[1]}
 
-        def load(n, h=None):
-            rows = src[n].rearrange("(m s) k -> m s k", s=4)
-            if h is None:
-                nc.sync.dma_start(out=raw[n][2], in_=rows)
-            else:
-                nc.sync.dma_start(out=raw[n][h], in_=rows[:, 2 * h : 2 * h + 2, :])
+        def load(n, h):
+            rows = src[n].rearrange("(m s) k -> m (s k)", s=4)
+            nc.sync.dma_start(out=raw[n][h], in_=rows[:, 2 * K * h : 2 * K * (h + 1)])
 
-        def load_bytes(b, lo=0, hi=4):
-            nc.sync.dma_start(out=xbytes[b][:, K * lo : K * hi], in_=x_re_bytes[b].rearrange("(m s) k -> m (s k)", s=4)[:, K * lo : K * hi])
+        def load_whole(n):
+            nc.sync.dma_start(out=whole[n][:], in_=src[n].rearrange("(m s) k -> m (s k)", s=4))
 
-        def load_scale(queue):
-            queue.dma_start(out=scale_col[:], in_=x_re_scale.rearrange("a b (p j) -> (a b p) j", j=4))
+        def load_bytes(b, h):
+            rows = x_re_bytes[b].rearrange("(m s) k -> m (s k)", s=4)
+            nc.sync.dma_start(out=xbytes[b][h][:], in_=rows[:, 2 * K * h : 2 * K * (h + 1)])
+
+        def load_scale():
+            nc.scalar.dma_start(out=scale_col[:], in_=x_re_scale.rearrange("a b (p j) -> (a b p) j", j=4))
 
         def load_bias(n):
             nc.sync.dma_start(out=bias[n][:], in_=bias_in[n].rearrange("(p t) -> p t", t=4))
 
-        def widen(b, h, engine="vector"):
-            source = xbytes[b][:, 2 * K * h : 2 * K * (h + 1)].bitcast(FP8)
-            target = raw["xr%d" % b][h].rearrange("p c k -> p (c k)")
+        def widen(b, h):
+            nc.vector.tensor_scalar(
+                out=raw["xr%d" % b][h].rearrange("p (u r e) -> p r u e", u=2, e=2),
+                in0=xbytes[b][h][:].bitcast(FP8).rearrange("p (r u e) -> p r u e", u=2, e=2),
+                scalar1=one[:],
+                scalar2=None,
+                op0=ALU.mult,
+            )
+
+        def sort(n, h, engine):
+            target = ordered[n][h][:].rearrange("p (u r e) -> p r u e", u=2, e=2)
+            source = raw[n][h].rearrange("p (r u e) -> p r u e", u=2, e=2)
             if engine == "scalar":
                 nc.scalar.copy(out=target, in_=source)
             else:
@@ -93,14 +108,19 @@ def tile_teleportationattention_pa_kernel(
 
         turned = {}
 
-        def turn(n, h):
-            bank = bank_tile()
+        def turn(n, h, j):
+            bank = bank_tile(j)
             turned[n, h] = bank
             v = bank[:].rearrange("p (u c r) -> p u c r", c=2, u=2)
             for c in range(2):
-                words = raw[n][h][:, c, :].bitcast(F32)
                 for u in range(2):
-                    nc.tensor.transpose(v[:, u, c, :], words[:, u:256:2], ident[:])
+                    if n in ordered:
+                        words = ordered[n][h][:].bitcast(F32)[:, 256 * u + P * c : 256 * u + P * (c + 1)]
+                    elif n[:2] == "xr":
+                        words = raw[n][h].bitcast(F32)[:, 256 * u + P * c : 256 * u + P * (c + 1)]
+                    else:
+                        words = raw[n][h].bitcast(F32)[:, 256 * c + u : 256 * (c + 1) : 2]
+                    nc.tensor.transpose(v[:, u, c, :], words, ident[:])
 
         def gather(n, h, engine="scalar"):
             target = grouped[n][:, 1024 * h : 1024 * (h + 1)].bitcast(F32).rearrange("p (r u) -> p r u", u=2)
@@ -147,11 +167,14 @@ def tile_teleportationattention_pa_kernel(
 
         summed = {}
 
-        def project(n, t):
-            bank = bank_tile()
-            summed[n, t] = bank
-            for i, (w, x) in enumerate(operands(n)):
-                mm(bank[:], w, t, x, 0, 4, i == 0, i == 1)
+        def first_term(n, t, j):
+            summed[n, t] = bank_tile(j)
+            w, x = operands(n)[0]
+            mm(summed[n, t][:], w, t, x, 0, 4, True, False)
+
+        def second_term(n, t):
+            w, x = operands(n)[1]
+            mm(summed[n, t][:], w, t, x, 0, 4, False, True)
 
         def leave(n, t, engine="scalar"):
             plane = planes[n][:, t, :]
@@ -161,13 +184,14 @@ def tile_teleportationattention_pa_kernel(
             else:
                 nc.vector.tensor_scalar(out=plane, in0=summed[n, t][:], scalar1=column, scalar2=None, op0=ALU.add)
 
-        def unit(n, on_vector=()):
-            for t in range(4):
-                project(n, t)
-                leave(n, t, "vector" if t in on_vector else "scalar")
+        def unit(n, j0, ts=(0, 1, 2, 3)):
+            for t in ts:
+                first_term(n, t, (j0 + t) % 8)
+                second_term(n, t)
+                leave(n, t)
 
-        def project_slot(n, s):
-            bank = bank_tile()
+        def project_slot(n, s, j):
+            bank = bank_tile(j)
             summed[n, s] = bank
             for t in range(4):
                 for i, (w, x) in enumerate(operands(n)):
@@ -181,13 +205,11 @@ def tile_teleportationattention_pa_kernel(
                 op=ALU.add,
             )
 
-        def interleave(n, h, engine="vector"):
-            target = grouped[n][:, 1024 * h : 1024 * (h + 1)].rearrange("p (c i t) -> p c t i", i=4, t=4)
-            source = planes[n][:, :, 256 * h : 256 * (h + 1)].rearrange("p t (c i) -> p c t i", i=4)
-            if engine == "scalar":
-                nc.scalar.copy(out=target, in_=source)
-            else:
-                nc.vector.tensor_copy(out=target, in_=source)
+        def interleave(n, h):
+            nc.vector.tensor_copy(
+                out=grouped[n][:, 1024 * h : 1024 * (h + 1)].rearrange("p (c i t) -> p c t i", i=4, t=4),
+                in_=planes[n][:, :, 256 * h : 256 * (h + 1)].rearrange("p t (c i) -> p c t i", i=4),
+            )
 
         def interleave_whole(n):
             nc.vector.tensor_copy(
@@ -195,18 +217,12 @@ def tile_teleportationattention_pa_kernel(
                 in_=planes[n][:].rearrange("p t (c i) -> p c t i", i=4),
             )
 
-        def pack(n):
-            interleave(n, 0)
-            interleave(n, 1)
-            quant(n, 0, 2)
-            quant(n, 2, 4)
-
         scored = {}
 
-        def score(b, s, part, start):
-            if start:
-                scored[b, s] = bank_tile()
-            mm(scored[b, s][:], "q%s%d" % (part, b), s, "k%s%d" % (part, b), 0, 4, start, not start)
+        def score(b, s, j):
+            scored[b, s] = bank_tile(j)
+            for i, part in enumerate("ir"):
+                mm(scored[b, s][:], "q%s%d" % (part, b), s, "k%s%d" % (part, b), 0, 4, i == 0, i == 1)
 
         def store(b, s, engine="scalar"):
             o = result[b][s][:].rearrange("p (m j) -> p m j", j=4)
@@ -217,65 +233,72 @@ def tile_teleportationattention_pa_kernel(
                 nc.vector.tensor_copy(out=o, in_=i)
             nc.sync.dma_start(out=out[b].rearrange("(m s) k -> m s k", s=4)[:, s, :], in_=result[b][s][:])
 
+        def warm_up(count, j):
+            bank = bank_tile(j)
+            for i in range(count):
+                nc.tensor.matmul(bank[:], idle[:, 0:P], idle[:], start=True, stop=True)
+
         with tc.manual_schedule():
-            load_scale(nc.scalar)
+            load_scale()
             make_identity(nc, ident[:])
-            load_bytes(0, 0, 2)
+            nc.vector.memset(idle[:], 0.0)
+            nc.vector.memset(one[:], 1.0)
+            load_bytes(0, 0)
             load("xi0", 0)
-            load_bytes(0, 2, 4)
-            load_bytes(1, 0, 2)
+            load_bytes(0, 1)
+            load_bytes(1, 0)
             load("xi0", 1)
             load("wqr", 0)
-            load_bytes(1, 2, 4)
+            load_bytes(1, 1)
             load("wqr", 1)
-            load("wqi", 0)
-            load("wqi", 1)
-            load("wkr", 0)
-            load("wkr", 1)
-            load("wki", 0)
-            load("wki", 1)
-            load("xi1", 0)
-            load("xi1", 1)
-            load_bias("qi")
-            load_bias("ki")
-            load_bias("qr")
-            load_bias("kr")
-            nc.vector.memset(dummy[:], 0.0)
-            nc.scalar.activation(out=dummy[:], in_=dummy[:], func=ACT.Identity, bias=0.0, scale=1.0)
+            for n in ("wqi", "wkr", "wki", "xi1"):
+                load(n, 0)
+                load(n, 1)
+            for n in ("qi", "ki", "qr", "kr"):
+                load_bias(n)
 
+            warm_up(5, 7)
             widen(0, 0)
             widen(0, 1)
             widen(1, 0)
-            for h in range(2):
-                turn("xi0", h)
-                gather("xi0", h)
-                turn("xr0", h)
-                gather_scaled("xr0", h)
-            widen(1, 1)
-            turn("wqr", 0)
+            turn("xi0", 0, 0)
+            gather("xi0", 0)
+            turn("xr0", 0, 1)
+            gather_scaled("xr0", 0)
+            turn("xi0", 1, 2)
+            gather("xi0", 1)
+            turn("wqr", 0, 3)
             gather("wqr", 0)
-            turn("xr1", 0)
-            turn("wqr", 1)
+            turn("xr0", 1, 4)
+            gather_scaled("xr0", 1)
+            widen(1, 1)
+            turn("wqr", 1, 5)
             gather("wqr", 1)
             quant("xi0")
             quant("xr0")
-            turn("wqi", 0)
+            turn("wqi", 0, 6)
             gather("wqi", 0)
-            gather_scaled("xr1", 0)
-            turn("wqi", 1)
+            turn("wqi", 1, 7)
             gather("wqi", 1)
+            turn("xr1", 0, 0)
             quant("wqr")
-            turn("wkr", 0)
+            gather_scaled("xr1", 0)
+            turn("wkr", 0, 1)
             gather("wkr", 0)
-            turn("xr1", 1)
             quant("wqi")
-            gather_scaled("xr1", 1)
-            turn("wkr", 1)
+            turn("wkr", 1, 2)
             gather("wkr", 1)
-            for n in ("wki", "xi1"):
-                for h in range(2):
-                    turn(n, h)
-                    gather(n, h)
+            turn("wki", 0, 3)
+            gather("wki", 0)
+            turn("xr1", 1, 4)
+            gather_scaled("xr1", 1)
+            turn("wki", 1, 5)
+            gather("wki", 1)
+            turn("xi1", 0, 6)
+            gather("xi1", 0)
+            turn("xi1", 1, 7)
+            gather("xi1", 1)
+
             negate(0)
             quant("wkr")
             quant("wki")
@@ -286,24 +309,27 @@ def tile_teleportationattention_pa_kernel(
             quant("xn1")
             order = ("qi0", "ki0", "qr0", "kr0", "ki1", "kr1")
             for i, n in enumerate(order):
-                unit(n)
+                unit(n, 4 * (i % 2))
                 interleave_whole(n)
                 if i > 0:
                     quant(order[i - 1])
-            unit("qi1")
+            JB = 0
+
+            unit("qi1", JB)
             quant("kr1")
             for s in range(4):
-                score(0, s, "i", True)
-                score(0, s, "r", False)
+                score(0, s, (JB + 4 + s) % 8)
                 store(0, s)
-            pack("qi1")
+            interleave("qi1", 0)
+            interleave("qi1", 1)
+            quant("qi1", 0, 2)
+            quant("qi1", 2, 4)
             for s in range(4):
-                project_slot("qr1", s)
+                project_slot("qr1", s, (JB + s) % 8)
                 leave_slot("qr1", s)
                 if s > 0:
                     quant("qr1", s - 1, s)
             quant("qr1", 3, 4)
             for s in range(4):
-                score(1, s, "i", True)
-                score(1, s, "r", False)
+                score(1, s, (JB + 4 + s) % 8)
                 store(1, s, "vector" if s == 3 else "scalar")

@@ -17,7 +17,7 @@ ACT = mybir.ActivationFunctionType
 P = 128
 K = 512
 BATCHES = 2
-SORTED = ()
+SORTED = (("xr0", 1), ("xr1", 0), ("xr1", 1))
 WHOLE = ()
 
 
@@ -37,7 +37,6 @@ def tile_teleportationattention_pa_kernel(
 
         ident = new("ident", [P, P], F32)
         idle = new("idle", [P, 512], BF16)
-        one = new("one", [P, 1], F32)
         scale_col = new("scale_col", [P, 4], F32)
         bias_in = {"qr": bq_re, "qi": bq_im, "kr": bk_re, "ki": bk_im}
         bias = {}
@@ -54,8 +53,8 @@ def tile_teleportationattention_pa_kernel(
                 raw[n] = [whole[n][:, 2 * K * h : 2 * K * (h + 1)] for h in range(2)]
             else:
                 raw[n] = [new("raw_%s_%d" % (n, h), [P, 2 * K], BF16)[:] for h in range(2)]
-        for n in SORTED:
-            ordered[n] = [new("ord_%s_%d" % (n, h), [P, 2 * K], BF16) for h in range(2)]
+        for n, h in SORTED:
+            ordered[n, h] = new("ord_%s_%d" % (n, h), [P, K], F32)
         xbytes = [[new("xbytes%d_%d" % (b, h), [P, 2 * K], U8) for h in range(2)] for b in range(BATCHES)]
         projected = ("qr0", "qi0", "kr0", "ki0", "qr1", "qi1", "kr1", "ki1")
         grouped = {}
@@ -89,22 +88,18 @@ def tile_teleportationattention_pa_kernel(
         def load_bias(n):
             nc.sync.dma_start(out=bias[n][:], in_=bias_in[n].rearrange("(p t) -> p t", t=4))
 
-        def widen(b, h):
-            nc.vector.tensor_scalar(
-                out=raw["xr%d" % b][h].rearrange("p (u r e) -> p r u e", u=2, e=2),
-                in0=xbytes[b][h][:].bitcast(FP8).rearrange("p (r u e) -> p r u e", u=2, e=2),
-                scalar1=one[:],
-                scalar2=None,
-                op0=ALU.mult,
-            )
-
-        def sort(n, h, engine):
-            target = ordered[n][h][:].rearrange("p (u r e) -> p r u e", u=2, e=2)
-            source = raw[n][h].rearrange("p (r u e) -> p r u e", u=2, e=2)
+        def widen(b, h, engine):
+            source = xbytes[b][h][:].bitcast(FP8)
             if engine == "scalar":
-                nc.scalar.copy(out=target, in_=source)
+                nc.scalar.copy(out=raw["xr%d" % b][h], in_=source)
             else:
-                nc.vector.tensor_copy(out=target, in_=source)
+                nc.vector.tensor_copy(out=raw["xr%d" % b][h], in_=source)
+
+        def sort(n, h):
+            nc.vector.tensor_copy(
+                out=ordered[n, h][:].rearrange("p (u r) -> p u r", u=2),
+                in_=raw[n][h].bitcast(F32).rearrange("p (r u) -> p u r", u=2),
+            )
 
         turned = {}
 
@@ -114,10 +109,8 @@ def tile_teleportationattention_pa_kernel(
             v = bank[:].rearrange("p (u c r) -> p u c r", c=2, u=2)
             for c in range(2):
                 for u in range(2):
-                    if n in ordered:
-                        words = ordered[n][h][:].bitcast(F32)[:, 256 * u + P * c : 256 * u + P * (c + 1)]
-                    elif n[:2] == "xr":
-                        words = raw[n][h].bitcast(F32)[:, 256 * u + P * c : 256 * u + P * (c + 1)]
+                    if (n, h) in ordered:
+                        words = ordered[n, h][:, 256 * u + P * c : 256 * u + P * (c + 1)]
                     else:
                         words = raw[n][h].bitcast(F32)[:, 256 * c + u : 256 * (c + 1) : 2]
                     nc.tensor.transpose(v[:, u, c, :], words, ident[:])
@@ -190,6 +183,22 @@ def tile_teleportationattention_pa_kernel(
                 second_term(n, t)
                 leave(n, t)
 
+        def half_unit(n, h, j0):
+            for pair in range(2):
+                bank = bank_tile((j0 + pair) % 8)
+                for c in range(2):
+                    for i, (w, x) in enumerate(operands(n)):
+                        mm(bank[:, 256 * c : 256 * (c + 1)], w, 2 * pair + c, x, 2 * h, 2 * h + 2, i == 0, i == 1)
+                for c in range(2):
+                    t = 2 * pair + c
+                    nc.scalar.activation(
+                        out=planes[n][:, t, 256 * h : 256 * (h + 1)],
+                        in_=bank[:, 256 * c : 256 * (c + 1)],
+                        func=ACT.Identity,
+                        bias=bias[n[:2]][:, t : t + 1],
+                        scale=1.0,
+                    )
+
         def project_slot(n, s, j):
             bank = bank_tile(j)
             summed[n, s] = bank
@@ -233,103 +242,106 @@ def tile_teleportationattention_pa_kernel(
                 nc.vector.tensor_copy(out=o, in_=i)
             nc.sync.dma_start(out=out[b].rearrange("(m s) k -> m s k", s=4)[:, s, :], in_=result[b][s][:])
 
-        def warm_up(count, j):
+        def warm_up(count, j, moving):
             bank = bank_tile(j)
             for i in range(count):
-                nc.tensor.matmul(bank[:], idle[:, 0:P], idle[:], start=True, stop=True)
+                nc.tensor.matmul(bank[:], idle[:, 0:P], moving, start=True, stop=True)
 
         with tc.manual_schedule():
             load_scale()
             make_identity(nc, ident[:])
             nc.vector.memset(idle[:], 0.0)
-            nc.vector.memset(one[:], 1.0)
-            load_bytes(0, 0)
-            load("xi0", 0)
-            load_bytes(0, 1)
-            load_bytes(1, 0)
-            load("xi0", 1)
-            load("wqr", 0)
-            load_bytes(1, 1)
-            load("wqr", 1)
-            for n in ("wqi", "wkr", "wki", "xi1"):
+            for b in range(BATCHES):
+                load_bytes(b, 0)
+                load_bytes(b, 1)
+            for n in ("xi0", "wqr", "wqi", "wkr", "wki", "xi1"):
                 load(n, 0)
                 load(n, 1)
             for n in ("qi", "ki", "qr", "kr"):
                 load_bias(n)
-
-            warm_up(5, 7)
-            widen(0, 0)
-            widen(0, 1)
-            widen(1, 0)
-            turn("xi0", 0, 0)
-            gather("xi0", 0)
-            turn("xr0", 0, 1)
+            warm_up(4, 7, idle[:])
+            widen(0, 0, "vector")
+            widen(0, 1, "scalar")
+            widen(1, 0, "vector")
+            widen(1, 1, "scalar")
+            turn("xr0", 0, 0)
+            warm_up(1, 7, idle[:])
+            sort("xr0", 1)
             gather_scaled("xr0", 0)
+            sort("xr1", 0)
+            sort("xr1", 1)
+            turn("xi0", 0, 1)
+            gather("xi0", 0)
             turn("xi0", 1, 2)
             gather("xi0", 1)
             turn("wqr", 0, 3)
             gather("wqr", 0)
+            quant("xi0")
             turn("xr0", 1, 4)
             gather_scaled("xr0", 1)
-            widen(1, 1)
             turn("wqr", 1, 5)
             gather("wqr", 1)
-            quant("xi0")
+            negate(0)
             quant("xr0")
             turn("wqi", 0, 6)
             gather("wqi", 0)
             turn("wqi", 1, 7)
             gather("wqi", 1)
-            turn("xr1", 0, 0)
             quant("wqr")
+            turn("xr1", 0, 0)
             gather_scaled("xr1", 0)
+            quant("wqi")
+            quant("xn0")
             turn("wkr", 0, 1)
             gather("wkr", 0)
-            quant("wqi")
             turn("wkr", 1, 2)
             gather("wkr", 1)
             turn("wki", 0, 3)
             gather("wki", 0)
             turn("xr1", 1, 4)
-            gather_scaled("xr1", 1)
             turn("wki", 1, 5)
             gather("wki", 1)
             turn("xi1", 0, 6)
             gather("xi1", 0)
             turn("xi1", 1, 7)
             gather("xi1", 1)
-
-            negate(0)
+            gather_scaled("xr1", 1)
             quant("wkr")
             quant("wki")
-            quant("xn0")
             quant("xr1")
             negate(1)
             quant("xi1")
             quant("xn1")
-            order = ("qi0", "ki0", "qr0", "kr0", "ki1", "kr1")
+            order = ("qi0", "qr0", "ki0", "kr0", "ki1")
             for i, n in enumerate(order):
                 unit(n, 4 * (i % 2))
                 interleave_whole(n)
                 if i > 0:
                     quant(order[i - 1])
-            JB = 0
-
-            unit("qi1", JB)
+            quant("ki1")
+            unit("kr1", 4)
+            interleave_whole("kr1")
+            unit("qi1", 0)
             quant("kr1")
+            half_unit("qr1", 0, 4)
+            interleave_whole("qi1")
+            interleave("qr1", 0)
+            quant("qi1")
+            quant("qr1", 0, 2)
             for s in range(4):
-                score(0, s, (JB + 4 + s) % 8)
+                score(0, s, (6 + s) % 8)
                 store(0, s)
-            interleave("qi1", 0)
-            interleave("qi1", 1)
-            quant("qi1", 0, 2)
-            quant("qi1", 2, 4)
-            for s in range(4):
-                project_slot("qr1", s, (JB + s) % 8)
-                leave_slot("qr1", s)
-                if s > 0:
-                    quant("qr1", s - 1, s)
+            project_slot("qr1", 2, 2)
+            project_slot("qr1", 3, 3)
+            leave_slot("qr1", 2)
+            leave_slot("qr1", 3)
+            quant("qr1", 2, 3)
             quant("qr1", 3, 4)
-            for s in range(4):
-                score(1, s, (JB + 4 + s) % 8)
-                store(1, s, "vector" if s == 3 else "scalar")
+            score(1, 0, 4)
+            store(1, 0)
+            score(1, 1, 5)
+            store(1, 1)
+            score(1, 2, 6)
+            store(1, 2)
+            score(1, 3, 7)
+            store(1, 3, "vector")

@@ -17,7 +17,7 @@ ACT = mybir.ActivationFunctionType
 P = 128
 K = 512
 BATCHES = 2
-SORTED = (("xr0", 1), ("xr1", 0), ("xr1", 1))
+SORTED = (("wki", 0), ("wki", 1), ("xr1", 0), ("xr1", 1), ("xi1", 0), ("xi1", 1))
 WHOLE = ()
 
 
@@ -36,7 +36,6 @@ def tile_teleportationattention_pa_kernel(
             return psum.tile([P, 512], F32, name="bank%d" % j)
 
         ident = new("ident", [P, P], F32)
-        idle = new("idle", [P, 512], BF16)
         scale_col = new("scale_col", [P, 4], F32)
         bias_in = {"qr": bq_re, "qi": bq_im, "kr": bk_re, "ki": bk_im}
         bias = {}
@@ -177,11 +176,11 @@ def tile_teleportationattention_pa_kernel(
             else:
                 nc.vector.tensor_scalar(out=plane, in0=summed[n, t][:], scalar1=column, scalar2=None, op0=ALU.add)
 
-        def unit(n, j0, ts=(0, 1, 2, 3)):
-            for t in ts:
+        def unit(n, j0, on_vector=()):
+            for t in range(4):
                 first_term(n, t, (j0 + t) % 8)
                 second_term(n, t)
-                leave(n, t)
+                leave(n, t, "vector" if t in on_vector else "scalar")
 
         def half_unit(n, h, j0):
             for pair in range(2):
@@ -242,85 +241,100 @@ def tile_teleportationattention_pa_kernel(
                 nc.vector.tensor_copy(out=o, in_=i)
             nc.sync.dma_start(out=out[b].rearrange("(m s) k -> m s k", s=4)[:, s, :], in_=result[b][s][:])
 
-        def warm_up(count, j, moving):
-            bank = bank_tile(j)
-            for i in range(count):
-                nc.tensor.matmul(bank[:], idle[:, 0:P], moving, start=True, stop=True)
-
         with tc.manual_schedule():
             load_scale()
             make_identity(nc, ident[:])
-            nc.vector.memset(idle[:], 0.0)
-            for b in range(BATCHES):
-                load_bytes(b, 0)
-                load_bytes(b, 1)
-            for n in ("xi0", "wqr", "wqi", "wkr", "wki", "xi1"):
+            load_bytes(0, 0)
+            load_bytes(0, 1)
+            load_bytes(1, 1)
+            for n in ("xi0", "wqr", "wqi", "wkr", "wki"):
                 load(n, 0)
                 load(n, 1)
-            for n in ("qi", "ki", "qr", "kr"):
-                load_bias(n)
-            warm_up(4, 7, idle[:])
+            load_bytes(1, 0)
+            load_bias("qi")
+            load("xi1", 0)
+            load("xi1", 1)
+            load_bias("qr")
+            load_bias("ki")
+            load_bias("kr")
             widen(0, 0, "vector")
             widen(0, 1, "scalar")
-            widen(1, 0, "vector")
-            widen(1, 1, "scalar")
+            widen(1, 1, "vector")
             turn("xr0", 0, 0)
-            warm_up(1, 7, idle[:])
-            sort("xr0", 1)
             gather_scaled("xr0", 0)
-            sort("xr1", 0)
             sort("xr1", 1)
             turn("xi0", 0, 1)
             gather("xi0", 0)
-            turn("xi0", 1, 2)
-            gather("xi0", 1)
-            turn("wqr", 0, 3)
-            gather("wqr", 0)
-            quant("xi0")
-            turn("xr0", 1, 4)
+            turn("xr0", 1, 2)
             gather_scaled("xr0", 1)
+            turn("xi0", 1, 3)
+            gather("xi0", 1)
+            quant("xi0")
+            quant("xr0")
+            turn("wqr", 0, 4)
+            gather("wqr", 0)
             turn("wqr", 1, 5)
             gather("wqr", 1)
+            quant("wqr")
             negate(0)
-            quant("xr0")
             turn("wqi", 0, 6)
             gather("wqi", 0)
             turn("wqi", 1, 7)
             gather("wqi", 1)
-            quant("wqr")
-            turn("xr1", 0, 0)
-            gather_scaled("xr1", 0)
             quant("wqi")
             quant("xn0")
-            turn("wkr", 0, 1)
+            turn("wkr", 0, 0)
             gather("wkr", 0)
-            turn("wkr", 1, 2)
+            turn("wkr", 1, 1)
             gather("wkr", 1)
-            turn("wki", 0, 3)
-            gather("wki", 0)
-            turn("xr1", 1, 4)
-            turn("wki", 1, 5)
-            gather("wki", 1)
-            turn("xi1", 0, 6)
-            gather("xi1", 0)
-            turn("xi1", 1, 7)
-            gather("xi1", 1)
-            gather_scaled("xr1", 1)
+            widen(1, 0, "scalar")
+            for t in range(4):
+                first_term("qi0", t, 2 + t)
+            sort("wki", 0)
+            sort("wki", 1)
             quant("wkr")
+            sort("xr1", 0)
+            sort("xi1", 0)
+            sort("xi1", 1)
+            for t in range(4):
+                second_term("qi0", t)
+                leave("qi0", t)
+            turn("xr1", 1, 6)
+            gather_scaled("xr1", 1)
+            turn("wki", 0, 7)
+            gather("wki", 0)
+            turn("wki", 1, 0)
+            gather("wki", 1)
+            turn("xr1", 0, 1)
+            gather_scaled("xr1", 0)
+            turn("xi1", 0, 2)
+            gather("xi1", 0)
+            turn("xi1", 1, 3)
+            gather("xi1", 1)
             quant("wki")
+            for t, j in enumerate((4, 5, 6, 7)):
+                first_term("qr0", t, j)
+                second_term("qr0", t)
+                leave("qr0", t)
+            interleave_whole("qi0")
+            unit("ki0", 0)
             quant("xr1")
             negate(1)
             quant("xi1")
             quant("xn1")
-            order = ("qi0", "qr0", "ki0", "kr0", "ki1")
-            for i, n in enumerate(order):
-                unit(n, 4 * (i % 2))
-                interleave_whole(n)
-                if i > 0:
-                    quant(order[i - 1])
-            quant("ki1")
+            interleave_whole("qr0")
+            quant("qi0")
+            unit("kr0", 4)
+            interleave_whole("ki0")
+            quant("qr0")
+            interleave_whole("kr0")
+            quant("ki0")
+            unit("ki1", 0, (2,))
+            quant("kr0")
+            interleave_whole("ki1")
             unit("kr1", 4)
             interleave_whole("kr1")
+            quant("ki1")
             unit("qi1", 0)
             quant("kr1")
             half_unit("qr1", 0, 4)

@@ -18,7 +18,8 @@ P = 128
 K = 512
 BATCHES = 2
 SORTED = (("wki", 0), ("wki", 1), ("xr1", 0), ("xr1", 1), ("xi1", 0), ("xi1", 1))
-WHOLE = ()
+WHOLE = ("wki", "xi1")
+PAIRS = (("xi0",), ("xr0",), ("wqr",), ("wqi",), ("wkr",), ("wki",), ("xn0",), ("xr1",), ("xi1", "xn1"), ("qi0", "qr0"), ("ki0",), ("kr0",), ("ki1",), ("kr1",), ("qi1",), ("qr1",))
 
 
 def tile_teleportationattention_pa_kernel(
@@ -53,16 +54,31 @@ def tile_teleportationattention_pa_kernel(
             else:
                 raw[n] = [new("raw_%s_%d" % (n, h), [P, 2 * K], BF16)[:] for h in range(2)]
         for n, h in SORTED:
-            ordered[n, h] = new("ord_%s_%d" % (n, h), [P, K], F32)
+            if n in WHOLE:
+                if n not in ordered:
+                    ordered[n] = new("ord_" + n, [P, 2 * K], F32)
+                ordered[n, h] = ordered[n][:, K * h : K * (h + 1)]
+            else:
+                ordered[n, h] = new("ord_%s_%d" % (n, h), [P, K], F32)[:]
         xbytes = [[new("xbytes%d_%d" % (b, h), [P, 2 * K], U8) for h in range(2)] for b in range(BATCHES)]
         projected = ("qr0", "qi0", "kr0", "ki0", "qr1", "qi1", "kr1", "ki1")
         grouped = {}
         codes = {}
         scales = {}
-        for n in inputs + ("xn0", "xn1") + projected:
-            grouped[n] = new("grp_" + n, [P, 4 * 512], BF16)
-            codes[n] = new("codes_" + n, [P, 512], U32)
-            scales[n] = new("scales_" + n, [P, 512], U8)
+        paired = {}
+        for pair in PAIRS:
+            name = "_".join(pair)
+            width = 512 * len(pair)
+            tiles = (
+                new("grp_" + name, [P, 4 * width], BF16),
+                new("codes_" + name, [P, width], U32),
+                new("scales_" + name, [P, width], U8),
+            )
+            paired[pair[0]] = tiles
+            for i, n in enumerate(pair):
+                grouped[n] = tiles[0][:, 2048 * i : 2048 * (i + 1)]
+                codes[n] = tiles[1][:, 512 * i : 512 * (i + 1)]
+                scales[n] = tiles[2][:, 512 * i : 512 * (i + 1)]
         planes = {}
         for n in projected:
             planes[n] = new("planes_" + n, [P, 4, 512], BF16)
@@ -94,10 +110,18 @@ def tile_teleportationattention_pa_kernel(
             else:
                 nc.vector.tensor_copy(out=raw["xr%d" % b][h], in_=source)
 
-        def sort(n, h):
+        def sort(n, h, engine="vector"):
+            target = ordered[n, h].rearrange("p (u r) -> p u r", u=2)
+            source = raw[n][h].bitcast(F32).rearrange("p (r u) -> p u r", u=2)
+            if engine == "scalar":
+                nc.scalar.copy(out=target, in_=source)
+            else:
+                nc.vector.tensor_copy(out=target, in_=source)
+
+        def sort_whole(n):
             nc.vector.tensor_copy(
-                out=ordered[n, h][:].rearrange("p (u r) -> p u r", u=2),
-                in_=raw[n][h].bitcast(F32).rearrange("p (r u) -> p u r", u=2),
+                out=ordered[n][:].rearrange("p (h u r) -> p h u r", h=2, u=2),
+                in_=whole[n][:].bitcast(F32).rearrange("p (h r u) -> p h u r", h=2, u=2),
             )
 
         turned = {}
@@ -137,8 +161,12 @@ def tile_teleportationattention_pa_kernel(
                 in_=grouped[n][:, 4 * P * lo : 4 * P * hi],
             )
 
+        def quant_pair(n):
+            values, words, exponents = paired[n]
+            nc.vector.quantize_mx(out=words[:].bitcast(FP8X4), scales=exponents[:], in_=values[:])
+
         def negate(b):
-            nc.vector.tensor_scalar(out=grouped["xn%d" % b][:], in0=grouped["xi%d" % b][:], scalar1=-1.0, scalar2=None, op0=ALU.mult)
+            nc.vector.tensor_scalar(out=grouped["xn%d" % b], in0=grouped["xi%d" % b], scalar1=-1.0, scalar2=None, op0=ALU.mult)
 
         def mm(target, w, t, x, lo, hi, start, stop):
             nc.tensor.matmul_mx(
@@ -221,7 +249,7 @@ def tile_teleportationattention_pa_kernel(
 
         def interleave_whole(n):
             nc.vector.tensor_copy(
-                out=grouped[n][:].rearrange("p (c i t) -> p c t i", i=4, t=4),
+                out=grouped[n].rearrange("p (c i t) -> p c t i", i=4, t=4),
                 in_=planes[n][:].rearrange("p t (c i) -> p c t i", i=4),
             )
 
@@ -260,9 +288,9 @@ def tile_teleportationattention_pa_kernel(
             widen(0, 0, "vector")
             widen(0, 1, "scalar")
             widen(1, 1, "vector")
+            sort("xr1", 1, "scalar")
             turn("xr0", 0, 0)
             gather_scaled("xr0", 0)
-            sort("xr1", 1)
             turn("xi0", 0, 1)
             gather("xi0", 0)
             turn("xr0", 1, 2)
@@ -288,17 +316,18 @@ def tile_teleportationattention_pa_kernel(
             turn("wkr", 1, 1)
             gather("wkr", 1)
             widen(1, 0, "scalar")
+            first_term("qi0", 0, 2)
             for t in range(4):
-                first_term("qi0", t, 2 + t)
-            sort("wki", 0)
-            sort("wki", 1)
+                if t < 3:
+                    first_term("qi0", t + 1, 3 + t)
+                second_term("qi0", t)
+                if t < 3:
+                    leave("qi0", t)
+            sort_whole("wki")
             quant("wkr")
             sort("xr1", 0)
-            sort("xi1", 0)
-            sort("xi1", 1)
-            for t in range(4):
-                second_term("qi0", t)
-                leave("qi0", t)
+            sort_whole("xi1")
+            leave("qi0", 3, "vector")
             turn("xr1", 1, 6)
             gather_scaled("xr1", 1)
             turn("wki", 0, 7)
@@ -312,32 +341,27 @@ def tile_teleportationattention_pa_kernel(
             turn("xi1", 1, 3)
             gather("xi1", 1)
             quant("wki")
-            for t, j in enumerate((4, 5, 6, 7)):
-                first_term("qr0", t, j)
-                second_term("qr0", t)
-                leave("qr0", t)
             interleave_whole("qi0")
-            unit("ki0", 0)
-            quant("xr1")
+            unit("qr0", 4)
             negate(1)
-            quant("xi1")
-            quant("xn1")
+            quant("xr1")
+            quant_pair("xi1")
+            unit("ki0", 0)
             interleave_whole("qr0")
-            quant("qi0")
             unit("kr0", 4)
             interleave_whole("ki0")
-            quant("qr0")
+            quant_pair("qi0")
+            unit("ki1", 0)
             interleave_whole("kr0")
             quant("ki0")
-            unit("ki1", 0, (2,))
-            quant("kr0")
             interleave_whole("ki1")
+            quant("kr0")
             unit("kr1", 4)
+            unit("qi1", 0)
             interleave_whole("kr1")
             quant("ki1")
-            unit("qi1", 0)
-            quant("kr1")
             half_unit("qr1", 0, 4)
+            quant("kr1")
             interleave_whole("qi1")
             interleave("qr1", 0)
             quant("qi1")

@@ -275,10 +275,12 @@ def tile_teleportationattention_pa_kernel(
             load_bytes(0, 0)
             load_bytes(0, 1)
             load_bytes(1, 1)
-            for n in ("xi0", "wqr", "wqi", "wkr", "wki"):
+            for n in ("xi0", "wqr", "wqi", "wkr"):
                 load(n, 0)
                 load(n, 1)
             load_bytes(1, 0)
+            load("wki", 0)
+            load("wki", 1)
             load_bias("qi")
             load("xi1", 0)
             load("xi1", 1)
@@ -298,12 +300,13 @@ def tile_teleportationattention_pa_kernel(
             turn("xi0", 1, 3)
             gather("xi0", 1)
             quant("xi0")
-            quant("xr0")
             turn("wqr", 0, 4)
             gather("wqr", 0)
             turn("wqr", 1, 5)
             gather("wqr", 1)
-            quant("wqr")
+            quant("wqr", 0, 2)
+            quant("xr0")
+            quant("wqr", 2, 4)
             negate(0)
             turn("wqi", 0, 6)
             gather("wqi", 0)
@@ -311,21 +314,25 @@ def tile_teleportationattention_pa_kernel(
             gather("wqi", 1)
             quant("wqi")
             quant("xn0")
-            turn("wkr", 0, 0)
-            gather("wkr", 0)
-            turn("wkr", 1, 1)
-            gather("wkr", 1)
             widen(1, 0, "scalar")
-            first_term("qi0", 0, 2)
-            for t in range(4):
-                if t < 3:
-                    first_term("qi0", t + 1, 3 + t)
-                second_term("qi0", t)
-                if t < 3:
-                    leave("qi0", t)
+            first_term("qi0", 0, 0)
+            first_term("qi0", 1, 1)
+            turn("wkr", 0, 2)
+            gather("wkr", 0)
+            turn("wkr", 1, 3)
+            gather("wkr", 1)
+            second_term("qi0", 0)
+            leave("qi0", 0)
+            second_term("qi0", 1)
+            leave("qi0", 1)
+            first_term("qi0", 2, 4)
+            second_term("qi0", 2)
+            leave("qi0", 2)
+            first_term("qi0", 3, 5)
+            second_term("qi0", 3)
             sort_whole("wki")
-            quant("wkr")
             sort("xr1", 0)
+            quant("wkr")
             sort_whole("xi1")
             leave("qi0", 3, "vector")
             turn("xr1", 1, 6)
@@ -375,11 +382,6 @@ def tile_teleportationattention_pa_kernel(
             leave_slot("qr1", 3)
             quant("qr1", 2, 3)
             quant("qr1", 3, 4)
-            score(1, 0, 4)
-            store(1, 0)
-            score(1, 1, 5)
-            store(1, 1)
-            score(1, 2, 6)
-            store(1, 2)
-            score(1, 3, 7)
-            store(1, 3, "vector")
+            for s in range(4):
+                score(1, s, (4 + s) % 8)
+                store(1, s, "vector" if s == 3 else "scalar")

@@ -17,9 +17,10 @@ ACT = mybir.ActivationFunctionType
 P = 128
 K = 512
 BATCHES = 2
-SORTED = (("wki", 0), ("wki", 1), ("xr1", 0), ("xr1", 1), ("xi1", 0), ("xi1", 1))
-WHOLE = ("wki", "xi1")
-PAIRS = (("xi0",), ("xr0",), ("wqr",), ("wqi",), ("wkr",), ("wki",), ("xn0",), ("xr1",), ("xi1", "xn1"), ("qi0", "qr0"), ("ki0",), ("kr0",), ("ki1",), ("kr1",), ("qi1",), ("qr1",))
+WEIGHTS = ("wqr", "wqi", "wkr", "wki")
+TOKENS = ("xr0", "xi0", "xr1", "xi1")
+REUSED = {"kr0": "ki0"}
+PROJECTED = ("qr0", "qi0", "ki0", "kr0", "qr1", "qi1", "kr1", "ki1")
 
 
 def tile_teleportationattention_pa_kernel(
@@ -36,6 +37,11 @@ def tile_teleportationattention_pa_kernel(
         def bank_tile(j):
             return psum.tile([P, 512], F32, name="bank%d" % j)
 
+        engines = {"scalar": nc.scalar.copy, "vector": nc.vector.tensor_copy, "gpsimd": nc.gpsimd.tensor_copy}
+
+        def copy(engine, target, source):
+            engines[engine](out=target, in_=source)
+
         ident = new("ident", [P, P], F32)
         scale_col = new("scale_col", [P, 4], F32)
         bias_in = {"qr": bq_re, "qi": bq_im, "kr": bk_re, "ki": bk_im}
@@ -43,59 +49,39 @@ def tile_teleportationattention_pa_kernel(
         for n in bias_in:
             bias[n] = new("bias_" + n, [P, 4], BF16)
 
-        inputs = ("wqr", "wqi", "wkr", "wki", "xr0", "xi0", "xr1", "xi1")
         raw = {}
         ordered = {}
-        whole = {}
-        for n in inputs:
-            if n in WHOLE:
-                whole[n] = new("raw_" + n, [P, 4 * K], BF16)
-                raw[n] = [whole[n][:, 2 * K * h : 2 * K * (h + 1)] for h in range(2)]
-            else:
-                raw[n] = [new("raw_%s_%d" % (n, h), [P, 2 * K], BF16)[:] for h in range(2)]
-        for n, h in SORTED:
-            if n in WHOLE:
-                if n not in ordered:
-                    ordered[n] = new("ord_" + n, [P, 2 * K], F32)
-                ordered[n, h] = ordered[n][:, K * h : K * (h + 1)]
-            else:
-                ordered[n, h] = new("ord_%s_%d" % (n, h), [P, K], F32)[:]
-        xbytes = [[new("xbytes%d_%d" % (b, h), [P, 2 * K], U8) for h in range(2)] for b in range(BATCHES)]
-        projected = ("qr0", "qi0", "kr0", "ki0", "qr1", "qi1", "kr1", "ki1")
+        for n in WEIGHTS + TOKENS:
+            for h in range(2):
+                raw[n, h] = new("raw_%s_%d" % (n, h), [P, 2 * K], BF16)
+        xbytes = {}
+        for b in range(BATCHES):
+            for h in range(2):
+                xbytes[b, h] = new("xbytes%d_%d" % (b, h), [P, 2 * K], U8)
         grouped = {}
         codes = {}
         scales = {}
-        paired = {}
-        for pair in PAIRS:
-            name = "_".join(pair)
-            width = 512 * len(pair)
-            tiles = (
-                new("grp_" + name, [P, 4 * width], BF16),
-                new("codes_" + name, [P, width], U32),
-                new("scales_" + name, [P, width], U8),
-            )
-            paired[pair[0]] = tiles
-            for i, n in enumerate(pair):
-                grouped[n] = tiles[0][:, 2048 * i : 2048 * (i + 1)]
-                codes[n] = tiles[1][:, 512 * i : 512 * (i + 1)]
-                scales[n] = tiles[2][:, 512 * i : 512 * (i + 1)]
+        for n in WEIGHTS + TOKENS + ("xn0", "xn1") + PROJECTED:
+            grouped[n] = grouped[REUSED[n]] if n in REUSED else new("grp_" + n, [P, 4 * K], BF16)
+            codes[n] = new("codes_" + n, [P, K], U32)
+            scales[n] = new("scales_" + n, [P, K], U8)
         planes = {}
-        for n in projected:
-            planes[n] = new("planes_" + n, [P, 4, 512], BF16)
-        result = [[new("result%d_%d" % (b, s), [P, 512], F32) for s in range(4)] for b in range(BATCHES)]
+        result = {}
 
-        src = {"wqr": Wq_re, "wqi": Wq_im, "wkr": Wk_re, "wki": Wk_im, "xi0": x_im[0], "xi1": x_im[1]}
+        weight_src = {"wqr": Wq_re, "wqi": Wq_im, "wkr": Wk_re, "wki": Wk_im}
+
+        def token_rows(source, h):
+            return source.rearrange("(h m r) k -> h m (r k)", h=2, r=2)[h]
 
         def load(n, h):
-            rows = src[n].rearrange("(m s) k -> m (s k)", s=4)
-            nc.sync.dma_start(out=raw[n][h], in_=rows[:, 2 * K * h : 2 * K * (h + 1)])
-
-        def load_whole(n):
-            nc.sync.dma_start(out=whole[n][:], in_=src[n].rearrange("(m s) k -> m (s k)", s=4))
+            if n in weight_src:
+                rows = weight_src[n].rearrange("(m t) k -> m (t k)", t=4)[:, 2 * K * h : 2 * K * (h + 1)]
+            else:
+                rows = token_rows(x_im[int(n[2])], h)
+            nc.sync.dma_start(out=raw[n, h][:], in_=rows)
 
         def load_bytes(b, h):
-            rows = x_re_bytes[b].rearrange("(m s) k -> m (s k)", s=4)
-            nc.sync.dma_start(out=xbytes[b][h][:], in_=rows[:, 2 * K * h : 2 * K * (h + 1)])
+            nc.sync.dma_start(out=xbytes[b, h][:], in_=token_rows(x_re_bytes[b], h))
 
         def load_scale():
             nc.scalar.dma_start(out=scale_col[:], in_=x_re_scale.rearrange("a b (p j) -> (a b p) j", j=4))
@@ -103,25 +89,15 @@ def tile_teleportationattention_pa_kernel(
         def load_bias(n):
             nc.sync.dma_start(out=bias[n][:], in_=bias_in[n].rearrange("(p t) -> p t", t=4))
 
-        def widen(b, h, engine):
-            source = xbytes[b][h][:].bitcast(FP8)
-            if engine == "scalar":
-                nc.scalar.copy(out=raw["xr%d" % b][h], in_=source)
-            else:
-                nc.vector.tensor_copy(out=raw["xr%d" % b][h], in_=source)
+        def widen(b, h, engine, lo=0, hi=2):
+            copy(engine, raw["xr%d" % b, h][:, K * lo : K * hi], xbytes[b, h][:, K * lo : K * hi].bitcast(FP8))
 
         def sort(n, h, engine="vector"):
-            target = ordered[n, h].rearrange("p (u r) -> p u r", u=2)
-            source = raw[n][h].bitcast(F32).rearrange("p (r u) -> p u r", u=2)
-            if engine == "scalar":
-                nc.scalar.copy(out=target, in_=source)
-            else:
-                nc.vector.tensor_copy(out=target, in_=source)
-
-        def sort_whole(n):
-            nc.vector.tensor_copy(
-                out=ordered[n][:].rearrange("p (h u r) -> p h u r", h=2, u=2),
-                in_=whole[n][:].bitcast(F32).rearrange("p (h r u) -> p h u r", h=2, u=2),
+            ordered[n, h] = new("ord_%s_%d" % (n, h), [P, K], F32)
+            copy(
+                engine,
+                ordered[n, h][:].rearrange("p (u r) -> p u r", u=2),
+                raw[n, h][:].bitcast(F32).rearrange("p (r u) -> p u r", u=2),
             )
 
         turned = {}
@@ -135,16 +111,15 @@ def tile_teleportationattention_pa_kernel(
                     if (n, h) in ordered:
                         words = ordered[n, h][:, 256 * u + P * c : 256 * u + P * (c + 1)]
                     else:
-                        words = raw[n][h].bitcast(F32)[:, 256 * c + u : 256 * (c + 1) : 2]
+                        words = raw[n, h][:].bitcast(F32)[:, 256 * c + u : 256 * (c + 1) : 2]
                     nc.tensor.transpose(v[:, u, c, :], words, ident[:])
 
         def gather(n, h, engine="scalar"):
-            target = grouped[n][:, 1024 * h : 1024 * (h + 1)].bitcast(F32).rearrange("p (r u) -> p r u", u=2)
-            source = turned[n, h][:].rearrange("p (u r) -> p r u", u=2)
-            if engine == "scalar":
-                nc.scalar.copy(out=target, in_=source)
-            else:
-                nc.vector.tensor_copy(out=target, in_=source)
+            copy(
+                engine,
+                grouped[n][:, 1024 * h : 1024 * (h + 1)].bitcast(F32).rearrange("p (r u) -> p r u", u=2),
+                turned[n, h][:].rearrange("p (u r) -> p r u", u=2),
+            )
 
         def gather_scaled(n, h):
             nc.vector.tensor_tensor(
@@ -161,12 +136,8 @@ def tile_teleportationattention_pa_kernel(
                 in_=grouped[n][:, 4 * P * lo : 4 * P * hi],
             )
 
-        def quant_pair(n):
-            values, words, exponents = paired[n]
-            nc.vector.quantize_mx(out=words[:].bitcast(FP8X4), scales=exponents[:], in_=values[:])
-
         def negate(b):
-            nc.vector.tensor_scalar(out=grouped["xn%d" % b], in0=grouped["xi%d" % b], scalar1=-1.0, scalar2=None, op0=ALU.mult)
+            nc.vector.tensor_scalar(out=grouped["xn%d" % b][:], in0=grouped["xi%d" % b][:], scalar1=-1.0, scalar2=None, op0=ALU.mult)
 
         def mm(target, w, t, x, lo, hi, start, stop):
             nc.tensor.matmul_mx(
@@ -196,7 +167,13 @@ def tile_teleportationattention_pa_kernel(
             w, x = operands(n)[1]
             mm(summed[n, t][:], w, t, x, 0, 4, False, True)
 
+        def project(n, t, j):
+            first_term(n, t, j)
+            second_term(n, t)
+
         def leave(n, t, engine="scalar"):
+            if n not in planes:
+                planes[n] = new("planes_" + n, [P, 4, 512], BF16)
             plane = planes[n][:, t, :]
             column = bias[n[:2]][:, t : t + 1]
             if engine == "scalar":
@@ -206,11 +183,12 @@ def tile_teleportationattention_pa_kernel(
 
         def unit(n, j0, on_vector=()):
             for t in range(4):
-                first_term(n, t, (j0 + t) % 8)
-                second_term(n, t)
+                project(n, t, (j0 + t) % 8)
                 leave(n, t, "vector" if t in on_vector else "scalar")
 
         def half_unit(n, h, j0):
+            if n not in planes:
+                planes[n] = new("planes_" + n, [P, 4, 512], BF16)
             for pair in range(2):
                 bank = bank_tile((j0 + pair) % 8)
                 for c in range(2):
@@ -241,33 +219,43 @@ def tile_teleportationattention_pa_kernel(
                 op=ALU.add,
             )
 
-        def interleave(n, h):
+        def interleave(n, lo=0, hi=4):
             nc.vector.tensor_copy(
-                out=grouped[n][:, 1024 * h : 1024 * (h + 1)].rearrange("p (c i t) -> p c t i", i=4, t=4),
-                in_=planes[n][:, :, 256 * h : 256 * (h + 1)].rearrange("p t (c i) -> p c t i", i=4),
+                out=grouped[n][:, 512 * lo : 512 * hi].rearrange("p (c i t) -> p c t i", i=4, t=4),
+                in_=planes[n][:, :, P * lo : P * hi].rearrange("p t (c i) -> p c t i", i=4),
             )
 
-        def interleave_whole(n):
-            nc.vector.tensor_copy(
-                out=grouped[n].rearrange("p (c i t) -> p c t i", i=4, t=4),
-                in_=planes[n][:].rearrange("p t (c i) -> p c t i", i=4),
+        def interleave_aside(n, lo=0, hi=4):
+            nc.gpsimd.tensor_scalar(
+                out=grouped[n][:, 512 * lo : 512 * hi].rearrange("p (c t) -> p c t", t=4),
+                in0=planes[n][:, :, P * lo : P * hi].rearrange("p t c -> p c t"),
+                scalar1=1.0,
+                scalar2=0.0,
+                op0=ALU.mult,
+                op1=ALU.add,
             )
 
         scored = {}
 
-        def score(b, s, j):
-            scored[b, s] = bank_tile(j)
-            for i, part in enumerate("ir"):
-                mm(scored[b, s][:], "q%s%d" % (part, b), s, "k%s%d" % (part, b), 0, 4, i == 0, i == 1)
+        def score_term(b, s, part, j, lo=0, hi=4):
+            if part == "i":
+                scored[b, s, lo] = bank_tile(j)
+            mm(scored[b, s, lo][:, : P * (hi - lo)], "q%s%d" % (part, b), s, "k%s%d" % (part, b), lo, hi, part == "i", part == "r")
 
-        def store(b, s, engine="scalar"):
-            o = result[b][s][:].rearrange("p (m j) -> p m j", j=4)
-            i = scored[b, s][:].rearrange("p (j m) -> p m j", j=4)
-            if engine == "scalar":
-                nc.scalar.copy(out=o, in_=i)
-            else:
-                nc.vector.tensor_copy(out=o, in_=i)
-            nc.sync.dma_start(out=out[b].rearrange("(m s) k -> m s k", s=4)[:, s, :], in_=result[b][s][:])
+        def score(b, s, j, lo=0, hi=4):
+            for part in "ir":
+                score_term(b, s, part, j, lo, hi)
+
+        def store(b, s, engine="scalar", lo=0, hi=4):
+            width = P * (hi - lo)
+            result[b, s, lo] = new("result%d_%d_%d" % (b, s, lo), [P, width], F32)
+            copy(
+                engine,
+                result[b, s, lo][:].rearrange("p (h m r) -> p h m r", r=2, m=P),
+                scored[b, s, lo][:, :width].rearrange("p (h r m) -> p h m r", r=2, m=P),
+            )
+            rows = out[b].rearrange("(h m r) k -> h r m k", h=2, r=2)[s // 2, s % 2]
+            nc.sync.dma_start(out=rows[:, P * lo : P * hi], in_=result[b, s, lo][:])
 
         with tc.manual_schedule():
             load_scale()
@@ -325,16 +313,17 @@ def tile_teleportationattention_pa_kernel(
             leave("qi0", 0)
             second_term("qi0", 1)
             leave("qi0", 1)
-            first_term("qi0", 2, 4)
-            second_term("qi0", 2)
+            project("qi0", 2, 4)
             leave("qi0", 2)
-            first_term("qi0", 3, 5)
-            second_term("qi0", 3)
-            sort_whole("wki")
+            project("qi0", 3, 5)
+            sort("wki", 0)
+            sort("wki", 1)
             sort("xr1", 0)
             quant("wkr")
-            sort_whole("xi1")
+            sort("xi1", 0)
+            sort("xi1", 1)
             leave("qi0", 3, "vector")
+            interleave_aside("qi0", 0, 3)
             turn("xr1", 1, 6)
             gather_scaled("xr1", 1)
             turn("wki", 0, 7)
@@ -348,29 +337,32 @@ def tile_teleportationattention_pa_kernel(
             turn("xi1", 1, 3)
             gather("xi1", 1)
             quant("wki")
-            interleave_whole("qi0")
+            interleave("qi0", 3, 4)
             unit("qr0", 4)
             negate(1)
             quant("xr1")
-            quant_pair("xi1")
+            quant("qi0")
+            quant("xi1")
+            quant("xn1")
             unit("ki0", 0)
-            interleave_whole("qr0")
+            interleave("qr0")
             unit("kr0", 4)
-            interleave_whole("ki0")
-            quant_pair("qi0")
-            unit("ki1", 0)
-            interleave_whole("kr0")
+            interleave("ki0")
+            quant("qr0")
             quant("ki0")
-            interleave_whole("ki1")
-            quant("kr0")
-            unit("kr1", 4)
+            unit("ki1", 0)
+            interleave_aside("kr0")
+            for s in range(4):
+                project_slot("kr1", s, 4 + s)
+                leave_slot("kr1", s)
             unit("qi1", 0)
-            interleave_whole("kr1")
-            quant("ki1")
+            interleave("ki1")
+            quant("kr0")
             half_unit("qr1", 0, 4)
             quant("kr1")
-            interleave_whole("qi1")
-            interleave("qr1", 0)
+            quant("ki1")
+            interleave("qi1")
+            interleave("qr1", 0, 2)
             quant("qi1")
             quant("qr1", 0, 2)
             for s in range(4):
@@ -382,6 +374,7 @@ def tile_teleportationattention_pa_kernel(
             leave_slot("qr1", 3)
             quant("qr1", 2, 3)
             quant("qr1", 3, 4)
-            for s in range(4):
-                score(1, s, (4 + s) % 8)
-                store(1, s, "vector" if s == 3 else "scalar")
+            for i in range(8):
+                s, lo = i // 2, 2 * (i % 2)
+                score(1, s, (4 + i) % 8, lo, lo + 2)
+                store(1, s, "vector" if i in (5, 7) else "scalar", lo, lo + 2)

@@ -19,8 +19,7 @@ K = 512
 BATCHES = 2
 WEIGHTS = ("wqr", "wqi", "wkr", "wki")
 TOKENS = ("xr0", "xi0", "xr1", "xi1")
-REUSED = {"kr0": "ki0"}
-PROJECTED = ("qr0", "qi0", "ki0", "kr0", "qr1", "qi1", "kr1", "ki1")
+PROJECTED = ("qr0", "qi0", "kr0", "ki0", "qr1", "qi1", "kr1", "ki1")
 
 
 def tile_teleportationattention_pa_kernel(
@@ -37,7 +36,7 @@ def tile_teleportationattention_pa_kernel(
         def bank_tile(j):
             return psum.tile([P, 512], F32, name="bank%d" % j)
 
-        engines = {"scalar": nc.scalar.copy, "vector": nc.vector.tensor_copy, "gpsimd": nc.gpsimd.tensor_copy}
+        engines = {"scalar": nc.scalar.copy, "vector": nc.vector.tensor_copy}
 
         def copy(engine, target, source):
             engines[engine](out=target, in_=source)
@@ -62,7 +61,7 @@ def tile_teleportationattention_pa_kernel(
         codes = {}
         scales = {}
         for n in WEIGHTS + TOKENS + ("xn0", "xn1") + PROJECTED:
-            grouped[n] = grouped[REUSED[n]] if n in REUSED else new("grp_" + n, [P, 4 * K], BF16)
+            grouped[n] = new("grp_" + n, [P, 4 * K], BF16)
             codes[n] = new("codes_" + n, [P, K], U32)
             scales[n] = new("scales_" + n, [P, K], U8)
         planes = {}
@@ -221,18 +220,8 @@ def tile_teleportationattention_pa_kernel(
 
         def interleave(n, lo=0, hi=4):
             nc.vector.tensor_copy(
-                out=grouped[n][:, 512 * lo : 512 * hi].rearrange("p (c i t) -> p c t i", i=4, t=4),
-                in_=planes[n][:, :, P * lo : P * hi].rearrange("p t (c i) -> p c t i", i=4),
-            )
-
-        def interleave_aside(n, lo=0, hi=4):
-            nc.gpsimd.tensor_scalar(
-                out=grouped[n][:, 512 * lo : 512 * hi].rearrange("p (c t) -> p c t", t=4),
-                in0=planes[n][:, :, P * lo : P * hi].rearrange("p t c -> p c t"),
-                scalar1=1.0,
-                scalar2=0.0,
-                op0=ALU.mult,
-                op1=ALU.add,
+                out=grouped[n][:, 512 * lo : 512 * hi].rearrange("p (c i t) -> p c t i", i=2, t=4),
+                in_=planes[n][:, :, P * lo : P * hi].rearrange("p t (c i) -> p c t i", i=2),
             )
 
         scored = {}
@@ -323,7 +312,6 @@ def tile_teleportationattention_pa_kernel(
             sort("xi1", 0)
             sort("xi1", 1)
             leave("qi0", 3, "vector")
-            interleave_aside("qi0", 0, 3)
             turn("xr1", 1, 6)
             gather_scaled("xr1", 1)
             turn("wki", 0, 7)
@@ -337,30 +325,29 @@ def tile_teleportationattention_pa_kernel(
             turn("xi1", 1, 3)
             gather("xi1", 1)
             quant("wki")
-            interleave("qi0", 3, 4)
+            interleave("qi0")
             unit("qr0", 4)
             negate(1)
             quant("xr1")
-            quant("qi0")
             quant("xi1")
             quant("xn1")
             unit("ki0", 0)
             interleave("qr0")
-            unit("kr0", 4)
+            unit("kr0", 4, (0,))
             interleave("ki0")
+            quant("qi0")
             quant("qr0")
-            quant("ki0")
             unit("ki1", 0)
-            interleave_aside("kr0")
-            for s in range(4):
-                project_slot("kr1", s, 4 + s)
-                leave_slot("kr1", s)
-            unit("qi1", 0)
+            interleave("kr0")
+            quant("ki0")
+            unit("kr1", 4)
             interleave("ki1")
             quant("kr0")
+            unit("qi1", 0)
+            interleave("kr1")
+            quant("ki1")
             half_unit("qr1", 0, 4)
             quant("kr1")
-            quant("ki1")
             interleave("qi1")
             interleave("qr1", 0, 2)
             quant("qi1")

@@ -19,7 +19,9 @@ K = 512
 BATCHES = 2
 WEIGHTS = ("wqr", "wqi", "wkr", "wki")
 TOKENS = ("xr0", "xi0", "xr1", "xi1")
-PROJECTED = ("qr0", "qi0", "kr0", "ki0", "qr1", "qi1", "kr1", "ki1")
+WHOLE = ("wki", "xi1")
+PLANES = (("qi0",), ("qr0",), ("ki0", "kr0"), ("ki1",), ("kr1",), ("qi1",), ("qr1",))
+GROUPS = (("xi0",), ("xr0",), ("wqr",), ("wqi",), ("wkr",), ("wki",), ("xn0",), ("xr1",), ("xi1", "xn1"), ("qi0", "qr0"), ("ki0", "kr0"), ("ki1", "kr1"), ("qi1",), ("qr1",))
 
 
 def tile_teleportationattention_pa_kernel(
@@ -51,8 +53,13 @@ def tile_teleportationattention_pa_kernel(
         raw = {}
         ordered = {}
         for n in WEIGHTS + TOKENS:
+            if n in WHOLE:
+                raw[n] = new("raw_" + n, [P, 4 * K], BF16)
             for h in range(2):
-                raw[n, h] = new("raw_%s_%d" % (n, h), [P, 2 * K], BF16)
+                if n in WHOLE:
+                    raw[n, h] = raw[n][:, 2 * K * h : 2 * K * (h + 1)]
+                else:
+                    raw[n, h] = new("raw_%s_%d" % (n, h), [P, 2 * K], BF16)
         xbytes = {}
         for b in range(BATCHES):
             for h in range(2):
@@ -60,11 +67,30 @@ def tile_teleportationattention_pa_kernel(
         grouped = {}
         codes = {}
         scales = {}
-        for n in WEIGHTS + TOKENS + ("xn0", "xn1") + PROJECTED:
-            grouped[n] = new("grp_" + n, [P, 4 * K], BF16)
-            codes[n] = new("codes_" + n, [P, K], U32)
-            scales[n] = new("scales_" + n, [P, K], U8)
         planes = {}
+        place = {}
+        for group in GROUPS:
+            name = "_".join(group)
+            width = K * len(group)
+            tiles = (
+                new("grp_" + name, [P, 4 * width], BF16),
+                new("codes_" + name, [P, width], U32),
+                new("scales_" + name, [P, width], U8),
+            )
+            for i, n in enumerate(group):
+                grouped[n], codes[n], scales[n] = tiles
+                place[n] = 4 * i
+        for group in PLANES:
+            flat = new("planes_" + "_".join(group), [P, 4, K * len(group)], BF16)
+            for i, n in enumerate(group):
+                planes[n] = flat[:, :, K * i :]
+
+        def values(n, lo=0, hi=4):
+            return grouped[n][:, 4 * P * (place[n] + lo) : 4 * P * (place[n] + hi)]
+
+        def columns(n, lo, hi):
+            return slice(P * (place[n] + lo), P * (place[n] + hi))
+
         result = {}
 
         weight_src = {"wqr": Wq_re, "wqi": Wq_im, "wkr": Wk_re, "wki": Wk_im}
@@ -99,6 +125,15 @@ def tile_teleportationattention_pa_kernel(
                 raw[n, h][:].bitcast(F32).rearrange("p (r u) -> p u r", u=2),
             )
 
+        def sort_whole(n):
+            both = new("ord_" + n, [P, 2 * K], F32)
+            nc.vector.tensor_copy(
+                out=both[:].rearrange("p (h u r) -> p h u r", h=2, u=2),
+                in_=raw[n][:].bitcast(F32).rearrange("p (h r u) -> p h u r", h=2, u=2),
+            )
+            for h in range(2):
+                ordered[n, h] = both[:, K * h : K * (h + 1)]
+
         turned = {}
 
         def turn(n, h, j):
@@ -116,13 +151,13 @@ def tile_teleportationattention_pa_kernel(
         def gather(n, h, engine="scalar"):
             copy(
                 engine,
-                grouped[n][:, 1024 * h : 1024 * (h + 1)].bitcast(F32).rearrange("p (r u) -> p r u", u=2),
+                values(n, 2 * h, 2 * h + 2).bitcast(F32).rearrange("p (r u) -> p r u", u=2),
                 turned[n, h][:].rearrange("p (u r) -> p r u", u=2),
             )
 
         def gather_scaled(n, h):
             nc.vector.tensor_tensor(
-                out=grouped[n][:, 1024 * h : 1024 * (h + 1)].rearrange("p (r u e) -> p r u e", u=2, e=2),
+                out=values(n, 2 * h, 2 * h + 2).rearrange("p (r u e) -> p r u e", u=2, e=2),
                 in0=turned[n, h][:].bitcast(BF16).rearrange("p (u r e) -> p r u e", u=2, e=2),
                 in1=scale_col[:].rearrange("p (u e) -> p u e", e=2).unsqueeze(1).to_broadcast([P, 256, 2, 2]),
                 op=ALU.mult,
@@ -130,21 +165,21 @@ def tile_teleportationattention_pa_kernel(
 
         def quant(n, lo=0, hi=4):
             nc.vector.quantize_mx(
-                out=codes[n][:, P * lo : P * hi].bitcast(FP8X4),
-                scales=scales[n][:, P * lo : P * hi],
-                in_=grouped[n][:, 4 * P * lo : 4 * P * hi],
+                out=codes[n][:, columns(n, lo, hi)].bitcast(FP8X4),
+                scales=scales[n][:, columns(n, lo, hi)],
+                in_=values(n, lo, hi),
             )
 
         def negate(b):
-            nc.vector.tensor_scalar(out=grouped["xn%d" % b][:], in0=grouped["xi%d" % b][:], scalar1=-1.0, scalar2=None, op0=ALU.mult)
+            nc.vector.tensor_scalar(out=values("xn%d" % b), in0=values("xi%d" % b), scalar1=-1.0, scalar2=None, op0=ALU.mult)
 
         def mm(target, w, t, x, lo, hi, start, stop):
             nc.tensor.matmul_mx(
                 out=target,
-                lhsT=codes[w][:, P * t : P * (t + 1)].bitcast(FP8X4),
-                lhsT_scale=scales[w][:, P * t : P * (t + 1)],
-                rhs=codes[x][:, P * lo : P * hi].bitcast(FP8X4),
-                rhs_scale=scales[x][:, P * lo : P * hi],
+                lhsT=codes[w][:, columns(w, t, t + 1)].bitcast(FP8X4),
+                lhsT_scale=scales[w][:, columns(w, t, t + 1)],
+                rhs=codes[x][:, columns(x, lo, hi)].bitcast(FP8X4),
+                rhs_scale=scales[x][:, columns(x, lo, hi)],
                 start=start,
                 stop=stop,
             )
@@ -171,9 +206,7 @@ def tile_teleportationattention_pa_kernel(
             second_term(n, t)
 
         def leave(n, t, engine="scalar"):
-            if n not in planes:
-                planes[n] = new("planes_" + n, [P, 4, 512], BF16)
-            plane = planes[n][:, t, :]
+            plane = planes[n][:, t, :K]
             column = bias[n[:2]][:, t : t + 1]
             if engine == "scalar":
                 nc.scalar.activation(out=plane, in_=summed[n, t][:], func=ACT.Identity, bias=column, scale=1.0)
@@ -186,8 +219,6 @@ def tile_teleportationattention_pa_kernel(
                 leave(n, t, "vector" if t in on_vector else "scalar")
 
         def half_unit(n, h, j0):
-            if n not in planes:
-                planes[n] = new("planes_" + n, [P, 4, 512], BF16)
             for pair in range(2):
                 bank = bank_tile((j0 + pair) % 8)
                 for c in range(2):
@@ -212,7 +243,7 @@ def tile_teleportationattention_pa_kernel(
 
         def leave_slot(n, s):
             nc.vector.tensor_tensor(
-                out=grouped[n][:, 512 * s : 512 * (s + 1)].rearrange("p (r t) -> p r t", t=4),
+                out=values(n, s, s + 1).rearrange("p (r t) -> p r t", t=4),
                 in0=summed[n, s][:].rearrange("p (t r) -> p r t", t=4),
                 in1=bias[n[:2]][:].unsqueeze(1).to_broadcast([P, P, 4]),
                 op=ALU.add,
@@ -220,8 +251,8 @@ def tile_teleportationattention_pa_kernel(
 
         def interleave(n, lo=0, hi=4):
             nc.vector.tensor_copy(
-                out=grouped[n][:, 512 * lo : 512 * hi].rearrange("p (c i t) -> p c t i", i=2, t=4),
-                in_=planes[n][:, :, P * lo : P * hi].rearrange("p t (c i) -> p c t i", i=2),
+                out=values(n, lo, hi).rearrange("p (c i t) -> p c t i", i=4, t=4),
+                in_=planes[n][:, :, P * lo : P * hi].rearrange("p t (c i) -> p c t i", i=4),
             )
 
         scored = {}
@@ -305,13 +336,11 @@ def tile_teleportationattention_pa_kernel(
             project("qi0", 2, 4)
             leave("qi0", 2)
             project("qi0", 3, 5)
-            sort("wki", 0)
-            sort("wki", 1)
+            sort_whole("wki")
             sort("xr1", 0)
+            sort_whole("xi1")
             quant("wkr")
-            sort("xi1", 0)
-            sort("xi1", 1)
-            leave("qi0", 3, "vector")
+            leave("qi0", 3)
             turn("xr1", 1, 6)
             gather_scaled("xr1", 1)
             turn("wki", 0, 7)
@@ -329,39 +358,49 @@ def tile_teleportationattention_pa_kernel(
             unit("qr0", 4)
             negate(1)
             quant("xr1")
-            quant("xi1")
-            quant("xn1")
+            quant("xi1", 0, 8)
             unit("ki0", 0)
             interleave("qr0")
-            unit("kr0", 4, (0,))
-            interleave("ki0")
+            half_unit("kr0", 0, 4)
+            project_slot("kr0", 2, 6)
+            project_slot("kr0", 3, 7)
             quant("qi0")
-            quant("qr0")
+            leave_slot("kr0", 2)
+            leave_slot("kr0", 3)
             unit("ki1", 0)
-            interleave("kr0")
-            quant("ki0")
+            quant("qr0")
+            interleave("ki0", 0, 6)
             unit("kr1", 4)
             interleave("ki1")
-            quant("kr0")
+            quant("ki0", 0, 8)
             unit("qi1", 0)
             interleave("kr1")
             quant("ki1")
             half_unit("qr1", 0, 4)
+            interleave("qi1", 0, 2)
             quant("kr1")
-            interleave("qi1")
             interleave("qr1", 0, 2)
-            quant("qi1")
+            quant("qi1", 0, 2)
             quant("qr1", 0, 2)
+            interleave("qi1", 2, 4)
             for s in range(4):
                 score(0, s, (6 + s) % 8)
                 store(0, s)
             project_slot("qr1", 2, 2)
             project_slot("qr1", 3, 3)
             leave_slot("qr1", 2)
-            leave_slot("qr1", 3)
+            quant("qi1", 2, 4)
             quant("qr1", 2, 3)
+            leave_slot("qr1", 3)
             quant("qr1", 3, 4)
-            for i in range(8):
-                s, lo = i // 2, 2 * (i % 2)
-                score(1, s, (4 + i) % 8, lo, lo + 2)
-                store(1, s, "vector" if i in (5, 7) else "scalar", lo, lo + 2)
+            for s in range(2):
+                score(1, s, 4 + s)
+                store(1, s)
+            for lo in (0, 2):
+                score(1, 2, lo // 2, lo, lo + 2)
+                store(1, 2, "scalar", lo, lo + 2)
+            for lo in (0, 2):
+                score_term(1, 3, "i", 2 + lo // 2, lo, lo + 2)
+            for lo, engine in ((0, "scalar"), (2, "vector")):
+                score_term(1, 3, "r", 2 + lo // 2, lo, lo + 2)
+                store(1, 3, engine, lo, lo + 2)

@@ -20,7 +20,7 @@ BATCHES = 2
 WEIGHTS = ("wqr", "wqi", "wkr", "wki")
 TOKENS = ("xr0", "xi0", "xr1", "xi1")
 WHOLE = ("wki", "xi1")
-PLANES = (("qi0",), ("qr0",), ("ki0", "kr0"), ("ki1",), ("kr1",), ("qi1",), ("qr1",))
+PLANES = (("qi0",), ("qr0",), ("ki0",), ("kr0",), ("ki1",), ("kr1",), ("qi1",), ("qr1",))
 GROUPS = (("xi0",), ("xr0",), ("wqr",), ("wqi",), ("wkr",), ("wki",), ("xn0",), ("xr1",), ("xi1", "xn1"), ("qi0", "qr0"), ("ki0", "kr0"), ("ki1", "kr1"), ("qi1",), ("qr1",))
 
 
@@ -255,6 +255,16 @@ def tile_teleportationattention_pa_kernel(
                 in_=planes[n][:, :, P * lo : P * hi].rearrange("p t (c i) -> p c t i", i=4),
             )
 
+        def interleave_aside(n, lo, hi):
+            nc.gpsimd.tensor_scalar(
+                out=values(n, lo, hi).rearrange("p (c t) -> p c t", t=4),
+                in0=planes[n][:, :, P * lo : P * hi].rearrange("p t c -> p c t"),
+                scalar1=1.0,
+                scalar2=0.0,
+                op0=ALU.mult,
+                op1=ALU.add,
+            )
+
         scored = {}
 
         def score_term(b, s, part, j, lo=0, hi=4):
@@ -340,7 +350,8 @@ def tile_teleportationattention_pa_kernel(
             sort("xr1", 0)
             sort_whole("xi1")
             quant("wkr")
-            leave("qi0", 3)
+            leave("qi0", 3, "vector")
+            interleave_aside("qi0", 0, 2)
             turn("xr1", 1, 6)
             gather_scaled("xr1", 1)
             turn("wki", 0, 7)
@@ -352,37 +363,33 @@ def tile_teleportationattention_pa_kernel(
             turn("xi1", 0, 2)
             gather("xi1", 0)
             turn("xi1", 1, 3)
-            gather("xi1", 1)
+            gather("xi1", 1, "vector")
             quant("wki")
-            interleave("qi0")
+            interleave("qi0", 2, 4)
             unit("qr0", 4)
             negate(1)
             quant("xr1")
             quant("xi1", 0, 8)
             unit("ki0", 0)
             interleave("qr0")
-            half_unit("kr0", 0, 4)
-            project_slot("kr0", 2, 6)
-            project_slot("kr0", 3, 7)
-            quant("qi0")
-            leave_slot("kr0", 2)
-            leave_slot("kr0", 3)
+            unit("kr0", 4)
+            interleave("ki0")
+            quant("qi0", 0, 8)
             unit("ki1", 0)
-            quant("qr0")
-            interleave("ki0", 0, 6)
+            interleave("kr0")
+            quant("ki0")
             unit("kr1", 4)
             interleave("ki1")
-            quant("ki0", 0, 8)
+            quant("kr0")
             unit("qi1", 0)
             interleave("kr1")
             quant("ki1")
             half_unit("qr1", 0, 4)
-            interleave("qi1", 0, 2)
             quant("kr1")
+            interleave("qi1")
             interleave("qr1", 0, 2)
             quant("qi1", 0, 2)
             quant("qr1", 0, 2)
-            interleave("qi1", 2, 4)
             for s in range(4):
                 score(0, s, (6 + s) % 8)
                 store(0, s)
@@ -393,9 +400,9 @@ def tile_teleportationattention_pa_kernel(
             quant("qr1", 2, 3)
             leave_slot("qr1", 3)
             quant("qr1", 3, 4)
-            for s in range(2):
-                score(1, s, 4 + s)
-                store(1, s)
+            for i in range(4):
+                score(1, i // 2, 4 + i, 2 * (i % 2), 2 * (i % 2) + 2)
+                store(1, i // 2, "scalar", 2 * (i % 2), 2 * (i % 2) + 2)
             for lo in (0, 2):
                 score(1, 2, lo // 2, lo, lo + 2)
                 store(1, 2, "scalar", lo, lo + 2)

@@ -21,7 +21,7 @@ WEIGHTS = ("wqr", "wqi", "wkr", "wki")
 TOKENS = ("xr0", "xi0", "xr1", "xi1")
 WHOLE = ("wki", "xi1")
 PLANES = (("qi0",), ("qr0",), ("ki0",), ("kr0",), ("ki1",), ("kr1",), ("qi1",), ("qr1",))
-GROUPS = (("xi0",), ("xr0",), ("wqr",), ("wqi",), ("wkr",), ("wki",), ("xn0",), ("xr1",), ("xi1", "xn1"), ("qi0", "qr0"), ("ki0", "kr0"), ("ki1", "kr1"), ("qi1",), ("qr1",))
+GROUPS = (("xi0",), ("xr0",), ("wqr",), ("wqi",), ("wkr",), ("wki",), ("xn0",), ("xr1",), ("xi1", "xn1"), ("qi0", "qr0"), ("ki0",), ("kr0",), ("ki1",), ("kr1",), ("qi1",), ("qr1",))
 
 
 def tile_teleportationattention_pa_kernel(
@@ -255,16 +255,6 @@ def tile_teleportationattention_pa_kernel(
                 in_=planes[n][:, :, P * lo : P * hi].rearrange("p t (c i) -> p c t i", i=4),
             )
 
-        def interleave_aside(n, lo, hi):
-            nc.gpsimd.tensor_scalar(
-                out=values(n, lo, hi).rearrange("p (c t) -> p c t", t=4),
-                in0=planes[n][:, :, P * lo : P * hi].rearrange("p t c -> p c t"),
-                scalar1=1.0,
-                scalar2=0.0,
-                op0=ALU.mult,
-                op1=ALU.add,
-            )
-
         scored = {}
 
         def score_term(b, s, part, j, lo=0, hi=4):
@@ -348,10 +338,9 @@ def tile_teleportationattention_pa_kernel(
             project("qi0", 3, 5)
             sort_whole("wki")
             sort("xr1", 0)
-            sort_whole("xi1")
             quant("wkr")
+            sort_whole("xi1")
             leave("qi0", 3, "vector")
-            interleave_aside("qi0", 0, 2)
             turn("xr1", 1, 6)
             gather_scaled("xr1", 1)
             turn("wki", 0, 7)
@@ -363,9 +352,9 @@ def tile_teleportationattention_pa_kernel(
             turn("xi1", 0, 2)
             gather("xi1", 0)
             turn("xi1", 1, 3)
-            gather("xi1", 1, "vector")
+            gather("xi1", 1)
             quant("wki")
-            interleave("qi0", 2, 4)
+            interleave("qi0")
             unit("qr0", 4)
             negate(1)
             quant("xr1")
@@ -388,7 +377,7 @@ def tile_teleportationattention_pa_kernel(
             quant("kr1")
             interleave("qi1")
             interleave("qr1", 0, 2)
-            quant("qi1", 0, 2)
+            quant("qi1")
             quant("qr1", 0, 2)
             for s in range(4):
                 score(0, s, (6 + s) % 8)
@@ -396,18 +385,10 @@ def tile_teleportationattention_pa_kernel(
             project_slot("qr1", 2, 2)
             project_slot("qr1", 3, 3)
             leave_slot("qr1", 2)
-            quant("qi1", 2, 4)
-            quant("qr1", 2, 3)
             leave_slot("qr1", 3)
+            quant("qr1", 2, 3)
             quant("qr1", 3, 4)
-            for i in range(4):
-                score(1, i // 2, 4 + i, 2 * (i % 2), 2 * (i % 2) + 2)
-                store(1, i // 2, "scalar", 2 * (i % 2), 2 * (i % 2) + 2)
-            for lo in (0, 2):
-                score(1, 2, lo // 2, lo, lo + 2)
-                store(1, 2, "scalar", lo, lo + 2)
-            for lo in (0, 2):
-                score_term(1, 3, "i", 2 + lo // 2, lo, lo + 2)
-            for lo, engine in ((0, "scalar"), (2, "vector")):
-                score_term(1, 3, "r", 2 + lo // 2, lo, lo + 2)
-                store(1, 3, engine, lo, lo + 2)
+            for i in range(8):
+                s, lo = i // 2, 2 * (i % 2)
+                score(1, s, (4 + i) % 8, lo, lo + 2)
+                store(1, s, "vector" if i in (5, 7) else "scalar", lo, lo + 2)

@@ -255,6 +255,16 @@ def tile_teleportationattention_pa_kernel(
                 in_=planes[n][:, :, P * lo : P * hi].rearrange("p t (c i) -> p c t i", i=4),
             )
 
+        def interleave_aside(n, lo, hi):
+            nc.gpsimd.tensor_scalar(
+                out=values(n, lo, hi).rearrange("p (c t) -> p c t", t=4),
+                in0=planes[n][:, :, P * lo : P * hi].rearrange("p t c -> p c t"),
+                scalar1=1.0,
+                scalar2=0.0,
+                op0=ALU.mult,
+                op1=ALU.add,
+            )
+
         scored = {}
 
         def score_term(b, s, part, j, lo=0, hi=4):
@@ -341,6 +351,7 @@ def tile_teleportationattention_pa_kernel(
             quant("wkr")
             sort_whole("xi1")
             leave("qi0", 3, "vector")
+            interleave_aside("qi0", 0, 2)
             turn("xr1", 1, 6)
             gather_scaled("xr1", 1)
             turn("wki", 0, 7)
@@ -354,14 +365,14 @@ def tile_teleportationattention_pa_kernel(
             turn("xi1", 1, 3)
             gather("xi1", 1)
             quant("wki")
-            interleave("qi0")
+            interleave("qi0", 2, 4)
             unit("qr0", 4)
             negate(1)
             quant("xr1")
             quant("xi1", 0, 8)
             unit("ki0", 0)
             interleave("qr0")
-            unit("kr0", 4)
+            unit("kr0", 4, (0,))
             interleave("ki0")
             quant("qi0", 0, 8)
             unit("ki1", 0)

@@ -21,7 +21,7 @@ WEIGHTS = ("wqr", "wqi", "wkr", "wki")
 TOKENS = ("xr0", "xi0", "xr1", "xi1")
 WHOLE = ("wki", "xi1")
 PLANES = (("qi0",), ("qr0",), ("ki0",), ("kr0",), ("ki1",), ("kr1",), ("qi1",), ("qr1",))
-GROUPS = (("xi0",), ("xr0",), ("wqr",), ("wqi",), ("wkr",), ("wki",), ("xn0",), ("xr1",), ("xi1", "xn1"), ("qi0", "qr0"), ("ki0",), ("kr0",), ("ki1",), ("kr1",), ("qi1",), ("qr1",))
+GROUPS = (("xi0",), ("xr0",), ("wqr",), ("wqi",), ("wkr",), ("wki",), ("xn0",), ("xr1",), ("xi1", "xn1"), ("qi0", "qr0"), ("ki0", "kr0"), ("ki1",), ("kr1",), ("qi1",), ("qr1",))
 
 
 def tile_teleportationattention_pa_kernel(
@@ -377,10 +377,9 @@ def tile_teleportationattention_pa_kernel(
             quant("qi0", 0, 8)
             unit("ki1", 0)
             interleave("kr0")
-            quant("ki0")
             unit("kr1", 4)
             interleave("ki1")
-            quant("kr0")
+            quant("ki0", 0, 8)
             unit("qi1", 0)
             interleave("kr1")
             quant("ki1")
@@ -388,7 +387,7 @@ def tile_teleportationattention_pa_kernel(
             quant("kr1")
             interleave("qi1")
             interleave("qr1", 0, 2)
-            quant("qi1")
+            quant("qi1", 0, 3)
             quant("qr1", 0, 2)
             for s in range(4):
                 score(0, s, (6 + s) % 8)
@@ -398,6 +397,7 @@ def tile_teleportationattention_pa_kernel(
             leave_slot("qr1", 2)
             leave_slot("qr1", 3)
             quant("qr1", 2, 3)
+            quant("qi1", 3, 4)
             quant("qr1", 3, 4)
             for i in range(8):
                 s, lo = i // 2, 2 * (i % 2)

@@ -86,6 +86,8 @@ def tile_teleportationattention_pa_kernel(
                 planes[n] = flat[:, :, K * i :]
 
         def values(n, lo=0, hi=4):
+            if (n, lo) == ("qi1", 3):
+                return values("qi1", 0, 1)
             return grouped[n][:, 4 * P * (place[n] + lo) : 4 * P * (place[n] + hi)]
 
         def columns(n, lo, hi):
@@ -352,10 +354,10 @@ def tile_teleportationattention_pa_kernel(
             sort_whole("xi1")
             leave("qi0", 3, "vector")
             interleave_aside("qi0", 0, 2)
-            turn("xr1", 1, 6)
-            gather_scaled("xr1", 1)
-            turn("wki", 0, 7)
+            turn("wki", 0, 6)
             gather("wki", 0)
+            turn("xr1", 1, 7)
+            gather_scaled("xr1", 1)
             turn("wki", 1, 0)
             gather("wki", 1)
             turn("xr1", 0, 1)
@@ -385,9 +387,10 @@ def tile_teleportationattention_pa_kernel(
             quant("ki1")
             half_unit("qr1", 0, 4)
             quant("kr1")
-            interleave("qi1")
+            interleave("qi1", 0, 3)
             interleave("qr1", 0, 2)
             quant("qi1", 0, 3)
+            interleave_aside("qi1", 3, 4)
             quant("qr1", 0, 2)
             for s in range(4):
                 score(0, s, (6 + s) % 8)

from contextlib import ExitStack

import concourse.mybir as mybir
from concourse.masks import make_identity

FLOPS = 8 * 2 * 1024 * 512 * 512 + 2 * 2 * 2 * 512 * 512 * 512

F32 = mybir.dt.float32
BF16 = mybir.dt.bfloat16
U32 = mybir.dt.uint32
U8 = mybir.dt.uint8
FP8 = mybir.dt.float8_e4m3fn
FP8X4 = mybir.dt.float8_e4m3fn_x4
ALU = mybir.AluOpType
ACT = mybir.ActivationFunctionType

P = 128
K = 512
BATCHES = 2
WEIGHTS = ("wqr", "wqi", "wkr", "wki")
TOKENS = ("xr0", "xi0", "xr1", "xi1")
WHOLE = ("wki", "xi1")
PLANES = (("qi0",), ("qr0",), ("ki0",), ("kr0",), ("ki1",), ("kr1",), ("qi1",), ("qr1",))
GROUPS = (("xi0",), ("xr0",), ("wqr",), ("wqi",), ("wkr",), ("wki",), ("xn0",), ("xr1",), ("xi1", "xn1"), ("qi0", "qr0"), ("ki0", "kr0"), ("ki1",), ("kr1",), ("qi1",), ("qr1",))


def tile_teleportationattention_pa_kernel(
    tc, x_re_bytes, x_re_scale, x_im, Wq_re, Wq_im, bq_re, bq_im, Wk_re, Wk_im, bk_re, bk_im, out
):
    nc = tc.nc
    with ExitStack() as ctx:
        keep = ctx.enter_context(tc.tile_pool(name="keep", bufs=1))
        psum = ctx.enter_context(tc.psum_pool(name="psum", bufs=1))

        def new(name, shape, dtype):
            return keep.tile(shape, dtype, name=name, align_bytes=256)

        def bank_tile(j):
            return psum.tile([P, 512], F32, name="bank%d" % j)

        engines = {"scalar": nc.scalar.copy, "vector": nc.vector.tensor_copy}

        def copy(engine, target, source):
            engines[engine](out=target, in_=source)

        ident = new("ident", [P, P], F32)
        scale_col = new("scale_col", [P, 4], F32)
        bias_in = {"qr": bq_re, "qi": bq_im, "kr": bk_re, "ki": bk_im}
        bias = {}
        for n in bias_in:
            bias[n] = new("bias_" + n, [P, 4], BF16)

        raw = {}
        ordered = {}
        for n in WEIGHTS + TOKENS:
            if n in WHOLE:
                raw[n] = new("raw_" + n, [P, 4 * K], BF16)
            for h in range(2):
                if n in WHOLE:
                    raw[n, h] = raw[n][:, 2 * K * h : 2 * K * (h + 1)]
                else:
                    raw[n, h] = new("raw_%s_%d" % (n, h), [P, 2 * K], BF16)
        xbytes = {}
        for b in range(BATCHES):
            for h in range(2):
                xbytes[b, h] = new("xbytes%d_%d" % (b, h), [P, 2 * K], U8)
        grouped = {}
        codes = {}
        scales = {}
        planes = {}
        place = {}
        for group in GROUPS:
            name = "_".join(group)
            width = K * len(group)
            tiles = (
                new("grp_" + name, [P, 4 * width], BF16),
                new("codes_" + name, [P, width], U32),
                new("scales_" + name, [P, width], U8),
            )
            for i, n in enumerate(group):
                grouped[n], codes[n], scales[n] = tiles
                place[n] = 4 * i
        for group in PLANES:
            flat = new("planes_" + "_".join(group), [P, 4, K * len(group)], BF16)
            for i, n in enumerate(group):
                planes[n] = flat[:, :, K * i :]

        def values(n, lo=0, hi=4):
            if (n, lo) == ("qi1", 3):
                return values("qi1", 0, 1)
            return grouped[n][:, 4 * P * (place[n] + lo) : 4 * P * (place[n] + hi)]

        def columns(n, lo, hi):
            return slice(P * (place[n] + lo), P * (place[n] + hi))

        result = {}

        weight_src = {"wqr": Wq_re, "wqi": Wq_im, "wkr": Wk_re, "wki": Wk_im}

        def token_rows(source, h):
            return source.rearrange("(h m r) k -> h m (r k)", h=2, r=2)[h]

        def load(n, h):
            if n in weight_src:
                rows = weight_src[n].rearrange("(m t) k -> m (t k)", t=4)[:, 2 * K * h : 2 * K * (h + 1)]
            else:
                rows = token_rows(x_im[int(n[2])], h)
            nc.sync.dma_start(out=raw[n, h][:], in_=rows)

        def load_bytes(b, h):
            nc.sync.dma_start(out=xbytes[b, h][:], in_=token_rows(x_re_bytes[b], h))

        def load_scale():
            nc.scalar.dma_start(out=scale_col[:], in_=x_re_scale.rearrange("a b (p j) -> (a b p) j", j=4))

        def load_bias(n):
            nc.sync.dma_start(out=bias[n][:], in_=bias_in[n].rearrange("(p t) -> p t", t=4))

        def widen(b, h, engine, lo=0, hi=2):
            copy(engine, raw["xr%d" % b, h][:, K * lo : K * hi], xbytes[b, h][:, K * lo : K * hi].bitcast(FP8))

        def sort(n, h, engine="vector"):
            ordered[n, h] = new("ord_%s_%d" % (n, h), [P, K], F32)
            copy(
                engine,
                ordered[n, h][:].rearrange("p (u r) -> p u r", u=2),
                raw[n, h][:].bitcast(F32).rearrange("p (r u) -> p u r", u=2),
            )

        def sort_whole(n):
            both = new("ord_" + n, [P, 2 * K], F32)
            nc.vector.tensor_copy(
                out=both[:].rearrange("p (h u r) -> p h u r", h=2, u=2),
                in_=raw[n][:].bitcast(F32).rearrange("p (h r u) -> p h u r", h=2, u=2),
            )
            for h in range(2):
                ordered[n, h] = both[:, K * h : K * (h + 1)]

        turned = {}

        def turn(n, h, j):
            bank = bank_tile(j)
            turned[n, h] = bank
            v = bank[:].rearrange("p (u c r) -> p u c r", c=2, u=2)
            for c in range(2):
                for u in range(2):
                    if (n, h) in ordered:
                        words = ordered[n, h][:, 256 * u + P * c : 256 * u + P * (c + 1)]
                    else:
                        words = raw[n, h][:].bitcast(F32)[:, 256 * c + u : 256 * (c + 1) : 2]
                    nc.tensor.transpose(v[:, u, c, :], words, ident[:])

        def gather(n, h, engine="scalar"):
            copy(
                engine,
                values(n, 2 * h, 2 * h + 2).bitcast(F32).rearrange("p (r u) -> p r u", u=2),
                turned[n, h][:].rearrange("p (u r) -> p r u", u=2),
            )

        def gather_scaled(n, h):
            nc.vector.tensor_tensor(
                out=values(n, 2 * h, 2 * h + 2).rearrange("p (r u e) -> p r u e", u=2, e=2),
                in0=turned[n, h][:].bitcast(BF16).rearrange("p (u r e) -> p r u e", u=2, e=2),
                in1=scale_col[:].rearrange("p (u e) -> p u e", e=2).unsqueeze(1).to_broadcast([P, 256, 2, 2]),
                op=ALU.mult,
            )

        def quant(n, lo=0, hi=4):
            nc.vector.quantize_mx(
                out=codes[n][:, columns(n, lo, hi)].bitcast(FP8X4),
                scales=scales[n][:, columns(n, lo, hi)],
                in_=values(n, lo, hi),
            )

        def negate(b):
            nc.vector.tensor_scalar(out=values("xn%d" % b), in0=values("xi%d" % b), scalar1=-1.0, scalar2=None, op0=ALU.mult)

        def mm(target, w, t, x, lo, hi, start, stop):
            nc.tensor.matmul_mx(
                out=target,
                lhsT=codes[w][:, columns(w, t, t + 1)].bitcast(FP8X4),
                lhsT_scale=scales[w][:, columns(w, t, t + 1)],
                rhs=codes[x][:, columns(x, lo, hi)].bitcast(FP8X4),
                rhs_scale=scales[x][:, columns(x, lo, hi)],
                start=start,
                stop=stop,
            )

        def operands(n):
            side, part, b = n
            if part == "r":
                return [("w%sr" % side, "xr" + b), ("w%si" % side, "xn" + b)]
            return [("w%sr" % side, "xi" + b), ("w%si" % side, "xr" + b)]

        summed = {}

        def first_term(n, t, j):
            summed[n, t] = bank_tile(j)
            w, x = operands(n)[0]
            mm(summed[n, t][:], w, t, x, 0, 4, True, False)

        def second_term(n, t):
            w, x = operands(n)[1]
            mm(summed[n, t][:], w, t, x, 0, 4, False, True)

        def project(n, t, j):
            first_term(n, t, j)
            second_term(n, t)

        def leave(n, t, engine="scalar"):
            plane = planes[n][:, t, :K]
            column = bias[n[:2]][:, t : t + 1]
            if engine == "scalar":
                nc.scalar.activation(out=plane, in_=summed[n, t][:], func=ACT.Identity, bias=column, scale=1.0)
            else:
                nc.vector.tensor_scalar(out=plane, in0=summed[n, t][:], scalar1=column, scalar2=None, op0=ALU.add)

        def unit(n, j0, on_vector=()):
            for t in range(4):
                project(n, t, (j0 + t) % 8)
                leave(n, t, "vector" if t in on_vector else "scalar")

        def half_unit(n, h, j0):
            for pair in range(2):
                bank = bank_tile((j0 + pair) % 8)
                for c in range(2):
                    for i, (w, x) in enumerate(operands(n)):
                        mm(bank[:, 256 * c : 256 * (c + 1)], w, 2 * pair + c, x, 2 * h, 2 * h + 2, i == 0, i == 1)
                for c in range(2):
                    t = 2 * pair + c
                    nc.scalar.activation(
                        out=planes[n][:, t, 256 * h : 256 * (h + 1)],
                        in_=bank[:, 256 * c : 256 * (c + 1)],
                        func=ACT.Identity,
                        bias=bias[n[:2]][:, t : t + 1],
                        scale=1.0,
                    )

        def project_slot(n, s, j):
            bank = bank_tile(j)
            summed[n, s] = bank
            for t in range(4):
                for i, (w, x) in enumerate(operands(n)):
                    mm(bank[:, P * t : P * (t + 1)], w, t, x, s, s + 1, i == 0, i == 1)

        def leave_slot(n, s):
            nc.vector.tensor_tensor(
                out=values(n, s, s + 1).rearrange("p (r t) -> p r t", t=4),
                in0=summed[n, s][:].rearrange("p (t r) -> p r t", t=4),
                in1=bias[n[:2]][:].unsqueeze(1).to_broadcast([P, P, 4]),
                op=ALU.add,
            )

        def interleave(n, lo=0, hi=4):
            nc.vector.tensor_copy(
                out=values(n, lo, hi).rearrange("p (c i t) -> p c t i", i=4, t=4),
                in_=planes[n][:, :, P * lo : P * hi].rearrange("p t (c i) -> p c t i", i=4),
            )

        def interleave_aside(n, lo, hi):
            nc.gpsimd.tensor_scalar(
                out=values(n, lo, hi).rearrange("p (c t) -> p c t", t=4),
                in0=planes[n][:, :, P * lo : P * hi].rearrange("p t c -> p c t"),
                scalar1=1.0,
                scalar2=0.0,
                op0=ALU.mult,
                op1=ALU.add,
            )

        scored = {}

        def score_term(b, s, part, j, lo=0, hi=4):
            if part == "i":
                scored[b, s, lo] = bank_tile(j)
            mm(scored[b, s, lo][:, : P * (hi - lo)], "q%s%d" % (part, b), s, "k%s%d" % (part, b), lo, hi, part == "i", part == "r")

        def score(b, s, j, lo=0, hi=4):
            for part in "ir":
                score_term(b, s, part, j, lo, hi)

        def store(b, s, engine="scalar", lo=0, hi=4):
            width = P * (hi - lo)
            result[b, s, lo] = new("result%d_%d_%d" % (b, s, lo), [P, width], F32)
            copy(
                engine,
                result[b, s, lo][:].rearrange("p (h m r) -> p h m r", r=2, m=P),
                scored[b, s, lo][:, :width].rearrange("p (h r m) -> p h m r", r=2, m=P),
            )
            rows = out[b].rearrange("(h m r) k -> h r m k", h=2, r=2)[s // 2, s % 2]
            nc.sync.dma_start(out=rows[:, P * lo : P * hi], in_=result[b, s, lo][:])

        with tc.manual_schedule():
            load_scale()
            make_identity(nc, ident[:])
            load_bytes(0, 0)
            load_bytes(0, 1)
            load_bytes(1, 1)
            for n in ("xi0", "wqr", "wqi", "wkr"):
                load(n, 0)
                load(n, 1)
            load_bytes(1, 0)
            load("wki", 0)
            load("wki", 1)
            load_bias("qi")
            load("xi1", 0)
            load("xi1", 1)
            load_bias("qr")
            load_bias("ki")
            load_bias("kr")
            widen(0, 0, "vector")
            widen(0, 1, "scalar")
            widen(1, 1, "vector")
            sort("xr1", 1, "scalar")
            turn("xr0", 0, 0)
            gather_scaled("xr0", 0)
            turn("xi0", 0, 1)
            gather("xi0", 0)
            turn("xr0", 1, 2)
            gather_scaled("xr0", 1)
            turn("xi0", 1, 3)
            gather("xi0", 1)
            quant("xi0")
            turn("wqr", 0, 4)
            gather("wqr", 0)
            turn("wqr", 1, 5)
            gather("wqr", 1)
            quant("wqr", 0, 2)
            quant("xr0")
            quant("wqr", 2, 4)
            negate(0)
            turn("wqi", 0, 6)
            gather("wqi", 0)
            turn("wqi", 1, 7)
            gather("wqi", 1)
            quant("wqi")
            quant("xn0")
            widen(1, 0, "scalar")
            first_term("qi0", 0, 0)
            first_term("qi0", 1, 1)
            turn("wkr", 0, 2)
            gather("wkr", 0)
            turn("wkr", 1, 3)
            gather("wkr", 1)
            second_term("qi0", 0)
            leave("qi0", 0)
            second_term("qi0", 1)
            leave("qi0", 1)
            project("qi0", 2, 4)
            leave("qi0", 2)
            project("qi0", 3, 5)
            sort_whole("wki")
            sort("xr1", 0)
            quant("wkr")
            sort_whole("xi1")
            leave("qi0", 3, "vector")
            interleave_aside("qi0", 0, 2)
            turn("wki", 0, 6)
            gather("wki", 0)
            turn("xr1", 1, 7)
            gather_scaled("xr1", 1)
            turn("wki", 1, 0)
            gather("wki", 1)
            turn("xr1", 0, 1)
            gather_scaled("xr1", 0)
            turn("xi1", 0, 2)
            gather("xi1", 0)
            turn("xi1", 1, 3)
            gather("xi1", 1)
            quant("wki")
            interleave("qi0", 2, 4)
            unit("qr0", 4)
            negate(1)
            quant("xr1")
            quant("xi1", 0, 8)
            unit("ki0", 0)
            interleave("qr0")
            unit("kr0", 4, (0,))
            interleave("ki0")
            quant("qi0", 0, 8)
            unit("ki1", 0)
            interleave("kr0")
            unit("kr1", 4)
            interleave("ki1")
            quant("ki0", 0, 8)
            unit("qi1", 0)
            interleave("kr1")
            quant("ki1")
            half_unit("qr1", 0, 4)
            quant("kr1")
            interleave("qi1", 0, 3)
            interleave("qr1", 0, 2)
            quant("qi1", 0, 3)
            interleave_aside("qi1", 3, 4)
            quant("qr1", 0, 2)
            for s in range(4):
                score(0, s, (6 + s) % 8)
                store(0, s)
            project_slot("qr1", 2, 2)
            project_slot("qr1", 3, 3)
            leave_slot("qr1", 2)
            leave_slot("qr1", 3)
            quant("qr1", 2, 3)
            quant("qi1", 3, 4)
            quant("qr1", 3, 4)
            for i in range(8):
                s, lo = i // 2, 2 * (i % 2)
                score(1, s, (4 + i) % 8, lo, lo + 2)
                store(1, s, "vector" if i in (5, 7) else "scalar", lo, lo + 2)
